import numpy as np
import ml_dtypes


def mxq(x, axis, fmt="e4m3"):
    dtype, down = {"e4m3": (ml_dtypes.float8_e4m3fn, 7), "e5m2": (ml_dtypes.float8_e5m2, 14)}[fmt]
    v = np.moveaxis(np.asarray(x, np.float32).astype(ml_dtypes.bfloat16).astype(np.float64), axis, -1)
    blocks = v.reshape(v.shape[:-1] + (-1, 32))
    amax = np.abs(blocks).max(-1, keepdims=True)
    byte = np.maximum(np.where(amax > 0, np.frexp(amax)[1] - 1 + 127, 0) - down, 1)
    scale = np.exp2(byte - 127.0)
    codes = (blocks / scale).astype(np.float32).astype(dtype).astype(np.float64)
    return np.moveaxis((codes * scale).reshape(v.shape), -1, axis)


WIDE = False


def mx_kscale(k):
    if not WIDE:
        return np.ones(k)
    levels = np.array([20, -20, 10, -10, 0])
    a = np.random.permutation(np.resize(levels, k // 512 * 4)).reshape(k // 512, 4)
    idx = np.arange(k)
    return np.exp2(a[idx // 512, idx % 128 // 32])


BF16 = ml_dtypes.bfloat16


def bf(x):
    return np.asarray(x, np.float32).astype(BF16)


def f64(x):
    return np.asarray(x).astype(np.float64)


B, HH, WW, E, NH, D = 1, 512, 4, 1024, 8, 128
KD = NH * D


def setup_inputs():
    u = mx_kscale(E)
    ret_w = np.random.standard_normal((B, HH, WW, NH, D)) * 0.9
    kv_h = np.random.standard_normal((B, WW, NH, D, D)) * 0.8
    Wo = np.random.standard_normal((E, KD)) * 0.3 / np.sqrt(KD) / u[:, None]
    bo = np.random.standard_normal(E) * 0.2
    g = np.random.standard_normal((B, HH * WW, E)) * np.exp2(np.random.randint(-12, 1, (B, HH * WW, 1))) * 8.0 * u
    return {"ret_w": bf(ret_w), "kv_h": bf(kv_h), "Wo": bf(Wo), "bo": bf(bo), "grad_out": bf(g)}


def reference(ret_w, kv_h, Wo, bo, grad_out):
    g = f64(grad_out).reshape(B * HH * WW, E)
    go = mxq(g, 1, "e5m2") @ mxq(f64(Wo), 0, "e4m3")
    go = go.reshape(B, HH, WW * NH, D).transpose(0, 2, 1, 3)
    gr = go @ f64(kv_h).reshape(B, WW * NH, D, D).transpose(0, 1, 3, 2)
    return gr.transpose(0, 2, 1, 3).reshape(B, HH, WW, NH, D)

@@ -1,0 +1,186 @@
+from contextlib import ExitStack
+
+import concourse.mybir as mybir
+from concourse.masks import make_identity
+
+F32 = mybir.dt.float32
+BF16 = mybir.dt.bfloat16
+U32 = mybir.dt.uint32
+U8 = mybir.dt.uint8
+E4M3_X4 = mybir.dt.float8_e4m3fn_x4
+E5M2_X4 = mybir.dt.float8_e5m2_x4
+
+P = 128
+PACK = 4
+PAIR = 2
+HALVES = PACK // PAIR
+K_PASS = P * PACK
+
+HEIGHT, WIDTH, HEADS, D = 512, 4, 8, 128
+K = 1024
+PASSES = K // K_PASS
+H_BLOCKS = HEIGHT // P
+
+PIECE_HEADS = 2
+PIECE_COLS = PIECE_HEADS * D
+PIECES = HEADS // PIECE_HEADS
+PIECES_AHEAD = 2
+PREPARE_AT_HEAD = 4
+STORE_HEADS = 2
+BANK_BLOCKS = 2
+
+FLOPS = 2 * HEIGHT * WIDTH * K * HEADS * D + 2 * HEIGHT * WIDTH * HEADS * D * D
+BYTES = 2 * (WIDTH * HEADS * D * D + K * HEADS * D + HEIGHT * WIDTH * K) + 4 * HEIGHT * WIDTH * HEADS * D
+
+
+def tile_linear_retention_pb_kernel(tc, ret_w, kv_h, Wo, bo, grad_out, out):
+    nc = tc.nc
+
+    g_rows = grad_out[0].rearrange("(hb p w) k -> w p hb k", hb=H_BLOCKS, p=P, w=WIDTH)
+    kv_rows = kv_h[0].rearrange("w n e f -> w e n f")
+    wo_rows = Wo.rearrange("(s u p e) c -> s u p e c", s=PASSES, u=HALVES, p=P, e=PAIR)
+    out_rows = out[0].rearrange("(hb p) w n e -> w p hb n e", hb=H_BLOCKS, p=P)
+
+    with ExitStack() as ctx:
+        ctx.enter_context(tc.manual_schedule())
+        keep = ctx.enter_context(tc.tile_pool(name="keep", bufs=1))
+        chunk_pool = ctx.enter_context(tc.tile_pool(name="chunk", bufs=2))
+        stream = ctx.enter_context(tc.tile_pool(name="stream", bufs=3))
+        psum_go = ctx.enter_context(tc.psum_pool(name="psum_go", bufs=2))
+        psum_out = ctx.enter_context(tc.psum_pool(name="psum_out", bufs=2))
+        psum_t = ctx.enter_context(tc.psum_pool(name="psum_t", bufs=4))
+
+        g_raw = [keep.tile([P, H_BLOCKS, K], BF16, name="g_raw%d" % w) for w in range(WIDTH)]
+        kv_raw = [keep.tile([P, HEADS, D], BF16, name="kv_raw%d" % w) for w in range(WIDTH)]
+        wo_raw = [keep.tile([P, PASSES, PACK, PIECE_COLS], BF16, name="wo_raw%d" % i) for i in range(PIECES)]
+
+        def load_wo(piece):
+            cols = slice(piece * PIECE_COLS, (piece + 1) * PIECE_COLS)
+            for s in range(PASSES):
+                for u in range(HALVES):
+                    nc.sync.dma_start(
+                        out=wo_raw[piece][:, s, PAIR * u : PAIR * (u + 1), :],
+                        in_=wo_rows[s, u, :, :, cols],
+                    )
+
+        nc.sync.dma_start(out=g_raw[0][:], in_=g_rows[0])
+        load_wo(0)
+        nc.sync.dma_start(out=kv_raw[0][:], in_=kv_rows[0])
+        for piece in range(1, PIECES):
+            load_wo(piece)
+        for w in range(1, WIDTH):
+            nc.sync.dma_start(out=g_raw[w][:], in_=g_rows[w])
+            nc.sync.dma_start(out=kv_raw[w][:], in_=kv_rows[w])
+
+        ident_f32 = keep.tile([P, P], F32, name="ident_f32")
+        make_identity(nc, ident_f32[:])
+        ident_bf16 = keep.tile([P, P], BF16, name="ident_bf16")
+        make_identity(nc, ident_bf16[:])
+
+        wo_codes = [keep.tile([P, PASSES, PIECE_COLS], U32, name="wo_codes%d" % i, align_bytes=64) for i in range(PIECES)]
+        wo_scales = [keep.tile([P, PASSES, PIECE_COLS], U8, name="wo_scales%d" % i, align_bytes=64) for i in range(PIECES)]
+
+        def prepare_wo(piece):
+            grouped = chunk_pool.tile([P, PASSES, PIECE_COLS, PACK], BF16, name="wo_grouped", align_bytes=64)
+            for s in range(PASSES):
+                nc.vector.tensor_copy(
+                    out=grouped[:, s, :, :].rearrange("p (c i) t -> p c t i", i=4),
+                    in_=wo_raw[piece][:, s, :, :].rearrange("p t (c i) -> p c t i", i=4),
+                )
+            nc.vector.quantize_mx(
+                out=wo_codes[piece][:].rearrange("p s c -> p (s c)").bitcast(E4M3_X4),
+                scales=wo_scales[piece][:].rearrange("p s c -> p (s c)"),
+                in_=grouped[:].rearrange("p s c t -> p (s c t)"),
+            )
+
+        chunk = {}
+
+        def prepare_chunk(w):
+            grouped = chunk_pool.tile([P, PASSES, HEIGHT * PACK], BF16, name="g_grouped", align_bytes=64)
+            for s in range(PASSES):
+                words = grouped[:, s, :].bitcast(F32).rearrange("p (r u) -> p r u", u=HALVES)
+                for bank in range(H_BLOCKS // BANK_BLOCKS):
+                    xt = psum_t.tile([P, HALVES, BANK_BLOCKS * P], F32, name="xt", tag="t")
+                    for u in range(HALVES):
+                        first = (s * HALVES + u) * P
+                        for b in range(BANK_BLOCKS):
+                            nc.tensor.transpose(
+                                xt[:, u, b * P : (b + 1) * P],
+                                g_raw[w][:, bank * BANK_BLOCKS + b, :].bitcast(F32)[:, first : first + P],
+                                ident_f32[:],
+                            )
+                    tokens = slice(bank * BANK_BLOCKS * P, (bank + 1) * BANK_BLOCKS * P)
+                    if bank % 2 == 0:
+                        nc.scalar.copy(out=words[:, tokens, :], in_=xt[:].rearrange("p u r -> p r u"))
+                    else:
+                        nc.vector.tensor_copy(out=words[:, tokens, :], in_=xt[:].rearrange("p u r -> p r u"))
+
+            kt = psum_t.tile([P, HEADS, D], BF16, name="kt", tag="t")
+            for n in range(HEADS):
+                nc.tensor.transpose(kt[:, n, :], kv_raw[w][:, n, :], ident_bf16[:])
+            kv_t = chunk_pool.tile([P, HEADS, D], F32, name="kv_t")
+            nc.scalar.copy(out=kv_t[:], in_=kt[:])
+
+            codes = chunk_pool.tile([P, PASSES, HEIGHT], U32, name="g_codes", align_bytes=64)
+            scales = chunk_pool.tile([P, PASSES, HEIGHT], U8, name="g_scales", align_bytes=64)
+            for s in range(PASSES):
+                nc.vector.quantize_mx(
+                    out=codes[:, s, :].bitcast(E5M2_X4), scales=scales[:, s, :], in_=grouped[:, s, :]
+                )
+            chunk[w] = (codes, scales, kv_t)
+
+        def project(w, n):
+            codes, scales, kv_t = chunk[w]
+            piece = n // PIECE_HEADS
+            cols = slice((n % PIECE_HEADS) * D, (n % PIECE_HEADS + 1) * D)
+            go_ps = psum_go.tile([P, HEIGHT], F32, name="go_ps")
+            for s in range(PASSES):
+                nc.tensor.matmul_mx(
+                    out=go_ps[:],
+                    lhsT=wo_codes[piece][:, s, cols].bitcast(E4M3_X4),
+                    lhsT_scale=wo_scales[piece][:, s, cols],
+                    rhs=codes[:, s, :].bitcast(E5M2_X4),
+                    rhs_scale=scales[:, s, :],
+                    start=(s == 0),
+                    stop=(s == PASSES - 1),
+                )
+            go_sb = stream.tile([P, HEIGHT], F32, name="go_sb")
+            nc.scalar.copy(out=go_sb[:], in_=go_ps[:])
+            return go_sb
+
+        stores = {}
+
+        def read_out(w, n, go_sb):
+            codes, scales, kv_t = chunk[w]
+            out_ps = psum_out.tile([P, H_BLOCKS, D], F32, name="out_ps")
+            for hb in range(H_BLOCKS):
+                nc.tensor.matmul(
+                    out=out_ps[:, hb, :],
+                    lhsT=go_sb[:, hb * P : (hb + 1) * P],
+                    rhs=kv_t[:, n, :],
+                    start=True,
+                    stop=True,
+                )
+            if n % STORE_HEADS == 0:
+                stores[0] = stream.tile([P, H_BLOCKS, STORE_HEADS, D], F32, name="out_sb")
+            out_sb = stores[0]
+            nc.vector.tensor_copy(out=out_sb[:, :, n % STORE_HEADS, :], in_=out_ps[:])
+            if n % STORE_HEADS == STORE_HEADS - 1:
+                nc.sync.dma_start(out=out_rows[w, :, :, n + 1 - STORE_HEADS : n + 1, :], in_=out_sb[:])
+
+        steps = [(w, n) for w in range(WIDTH) for n in range(HEADS)]
+        prepare_chunk(0)
+        prepare_wo(0)
+        go_next = project(0, 0)
+        for piece in range(1, PIECES_AHEAD):
+            prepare_wo(piece)
+        for i in range(len(steps)):
+            w, n = steps[i]
+            go_now = go_next
+            if i + 1 < len(steps):
+                go_next = project(steps[i + 1][0], steps[i + 1][1])
+            read_out(w, n, go_now)
+            if w == 0 and n % PIECE_HEADS == 0 and n // PIECE_HEADS + PIECES_AHEAD < PIECES:
+                prepare_wo(n // PIECE_HEADS + PIECES_AHEAD)
+            if n == PREPARE_AT_HEAD and w + 1 < WIDTH:
+                prepare_chunk(w + 1)

@@ -26,7 +26,7 @@ PIECE_COLS = PIECE_HEADS * D
 PIECES = HEADS // PIECE_HEADS
 PIECES_AHEAD = 2
 PREPARE_AT_HEAD = 4
-STORE_HEADS = 2
+GO_PARTS = 2
 BANK_BLOCKS = 2
 
 FLOPS = 2 * HEIGHT * WIDTH * K * HEADS * D + 2 * HEIGHT * WIDTH * HEADS * D * D
@@ -45,7 +45,7 @@ def tile_linear_retention_pb_kernel(tc, ret_w, kv_h, Wo, bo, grad_out, out):
         ctx.enter_context(tc.manual_schedule())
         keep = ctx.enter_context(tc.tile_pool(name="keep", bufs=1))
         chunk_pool = ctx.enter_context(tc.tile_pool(name="chunk", bufs=2))
-        stream = ctx.enter_context(tc.tile_pool(name="stream", bufs=3))
+        stream = ctx.enter_context(tc.tile_pool(name="stream", bufs=4))
         psum_go = ctx.enter_context(tc.psum_pool(name="psum_go", bufs=2))
         psum_out = ctx.enter_context(tc.psum_pool(name="psum_out", bufs=2))
         psum_t = ctx.enter_context(tc.psum_pool(name="psum_t", bufs=4))
@@ -87,15 +87,17 @@ def tile_linear_retention_pb_kernel(tc, ret_w, kv_h, Wo, bo, grad_out, out):
                     out=grouped[:, s, :, :].rearrange("p (c i) t -> p c t i", i=4),
                     in_=wo_raw[piece][:, s, :, :].rearrange("p t (c i) -> p c t i", i=4),
                 )
-            nc.vector.quantize_mx(
-                out=wo_codes[piece][:].rearrange("p s c -> p (s c)").bitcast(E4M3_X4),
-                scales=wo_scales[piece][:].rearrange("p s c -> p (s c)"),
-                in_=grouped[:].rearrange("p s c t -> p (s c t)"),
-            )
+            for s in range(PASSES):
+                nc.vector.quantize_mx(
+                    out=wo_codes[piece][:, s, :].bitcast(E4M3_X4),
+                    scales=wo_scales[piece][:, s, :],
+                    in_=grouped[:, s, :, :].rearrange("p c t -> p (c t)"),
+                )
 
+        transposed = {}
         chunk = {}
 
-        def prepare_chunk(w):
+        def transpose_chunk(w):
             grouped = chunk_pool.tile([P, PASSES, HEIGHT * PACK], BF16, name="g_grouped", align_bytes=64)
             for s in range(PASSES):
                 words = grouped[:, s, :].bitcast(F32).rearrange("p (r u) -> p r u", u=HALVES)
@@ -110,17 +112,16 @@ def tile_linear_retention_pb_kernel(tc, ret_w, kv_h, Wo, bo, grad_out, out):
                                 ident_f32[:],
                             )
                     tokens = slice(bank * BANK_BLOCKS * P, (bank + 1) * BANK_BLOCKS * P)
-                    if bank % 2 == 0:
-                        nc.scalar.copy(out=words[:, tokens, :], in_=xt[:].rearrange("p u r -> p r u"))
-                    else:
-                        nc.vector.tensor_copy(out=words[:, tokens, :], in_=xt[:].rearrange("p u r -> p r u"))
-
+                    nc.scalar.copy(out=words[:, tokens, :], in_=xt[:].rearrange("p u r -> p r u"))
             kt = psum_t.tile([P, HEADS, D], BF16, name="kt", tag="t")
             for n in range(HEADS):
                 nc.tensor.transpose(kt[:, n, :], kv_raw[w][:, n, :], ident_bf16[:])
+            transposed[w] = (grouped, kt)
+
+        def finish_chunk(w):
+            grouped, kt = transposed[w]
             kv_t = chunk_pool.tile([P, HEADS, D], F32, name="kv_t")
             nc.scalar.copy(out=kv_t[:], in_=kt[:])
-
             codes = chunk_pool.tile([P, PASSES, HEIGHT], U32, name="g_codes", align_bytes=64)
             scales = chunk_pool.tile([P, PASSES, HEIGHT], U8, name="g_scales", align_bytes=64)
             for s in range(PASSES):
@@ -130,7 +131,7 @@ def tile_linear_retention_pb_kernel(tc, ret_w, kv_h, Wo, bo, grad_out, out):
             chunk[w] = (codes, scales, kv_t)
 
         def project(w, n):
-            codes, scales, kv_t = chunk[w]
+            codes, scales = chunk[w][0], chunk[w][1]
             piece = n // PIECE_HEADS
             cols = slice((n % PIECE_HEADS) * D, (n % PIECE_HEADS + 1) * D)
             go_ps = psum_go.tile([P, HEIGHT], F32, name="go_ps")
@@ -145,13 +146,13 @@ def tile_linear_retention_pb_kernel(tc, ret_w, kv_h, Wo, bo, grad_out, out):
                     stop=(s == PASSES - 1),
                 )
             go_sb = stream.tile([P, HEIGHT], F32, name="go_sb")
-            nc.scalar.copy(out=go_sb[:], in_=go_ps[:])
+            for part in range(GO_PARTS):
+                tokens = slice(part * HEIGHT // GO_PARTS, (part + 1) * HEIGHT // GO_PARTS)
+                nc.scalar.copy(out=go_sb[:, tokens], in_=go_ps[:, tokens])
             return go_sb
 
-        stores = {}
-
         def read_out(w, n, go_sb):
-            codes, scales, kv_t = chunk[w]
+            kv_t = chunk[w][2]
             out_ps = psum_out.tile([P, H_BLOCKS, D], F32, name="out_ps")
             for hb in range(H_BLOCKS):
                 nc.tensor.matmul(
@@ -161,16 +162,14 @@ def tile_linear_retention_pb_kernel(tc, ret_w, kv_h, Wo, bo, grad_out, out):
                     start=True,
                     stop=True,
                 )
-            if n % STORE_HEADS == 0:
-                stores[0] = stream.tile([P, H_BLOCKS, STORE_HEADS, D], F32, name="out_sb")
-            out_sb = stores[0]
-            nc.vector.tensor_copy(out=out_sb[:, :, n % STORE_HEADS, :], in_=out_ps[:])
-            if n % STORE_HEADS == STORE_HEADS - 1:
-                nc.sync.dma_start(out=out_rows[w, :, :, n + 1 - STORE_HEADS : n + 1, :], in_=out_sb[:])
+            out_sb = stream.tile([P, H_BLOCKS, D], F32, name="out_sb")
+            nc.vector.tensor_copy(out=out_sb[:], in_=out_ps[:])
+            nc.sync.dma_start(out=out_rows[w, :, :, n, :], in_=out_sb[:])
 
         steps = [(w, n) for w in range(WIDTH) for n in range(HEADS)]
-        prepare_chunk(0)
+        transpose_chunk(0)
         prepare_wo(0)
+        finish_chunk(0)
         go_next = project(0, 0)
         for piece in range(1, PIECES_AHEAD):
             prepare_wo(piece)
@@ -179,8 +178,10 @@ def tile_linear_retention_pb_kernel(tc, ret_w, kv_h, Wo, bo, grad_out, out):
             go_now = go_next
             if i + 1 < len(steps):
                 go_next = project(steps[i + 1][0], steps[i + 1][1])
+            if n == PREPARE_AT_HEAD + 1 and w + 1 < WIDTH:
+                finish_chunk(w + 1)
             read_out(w, n, go_now)
             if w == 0 and n % PIECE_HEADS == 0 and n // PIECE_HEADS + PIECES_AHEAD < PIECES:
                 prepare_wo(n // PIECE_HEADS + PIECES_AHEAD)
             if n == PREPARE_AT_HEAD and w + 1 < WIDTH:
-                prepare_chunk(w + 1)
+                transpose_chunk(w + 1)

@@ -28,6 +28,7 @@ PIECES_AHEAD = 2
 PREPARE_AT_HEAD = 4
 GO_PARTS = 2
 BANK_BLOCKS = 2
+BANKS = H_BLOCKS // BANK_BLOCKS
 
 FLOPS = 2 * HEIGHT * WIDTH * K * HEADS * D + 2 * HEIGHT * WIDTH * HEADS * D * D
 BYTES = 2 * (WIDTH * HEADS * D * D + K * HEADS * D + HEIGHT * WIDTH * K) + 4 * HEIGHT * WIDTH * HEADS * D
@@ -46,6 +47,7 @@ def tile_linear_retention_pb_kernel(tc, ret_w, kv_h, Wo, bo, grad_out, out):
         keep = ctx.enter_context(tc.tile_pool(name="keep", bufs=1))
         chunk_pool = ctx.enter_context(tc.tile_pool(name="chunk", bufs=2))
         stream = ctx.enter_context(tc.tile_pool(name="stream", bufs=4))
+        out_pool = ctx.enter_context(tc.tile_pool(name="out", bufs=8))
         psum_go = ctx.enter_context(tc.psum_pool(name="psum_go", bufs=2))
         psum_out = ctx.enter_context(tc.psum_pool(name="psum_out", bufs=2))
         psum_t = ctx.enter_context(tc.psum_pool(name="psum_t", bufs=4))
@@ -63,14 +65,21 @@ def tile_linear_retention_pb_kernel(tc, ret_w, kv_h, Wo, bo, grad_out, out):
                         in_=wo_rows[s, u, :, :, cols],
                     )
 
-        nc.sync.dma_start(out=g_raw[0][:], in_=g_rows[0])
+        def load_g(w):
+            for bank in range(BANKS):
+                blocks = slice(bank * BANK_BLOCKS, (bank + 1) * BANK_BLOCKS)
+                nc.sync.dma_start(out=g_raw[w][:, blocks, :], in_=g_rows[w, :, blocks, :])
+
+        def load_kv(w):
+            nc.sync.dma_start(out=kv_raw[w][:], in_=kv_rows[w])
+
+        load_g(0)
         load_wo(0)
-        nc.sync.dma_start(out=kv_raw[0][:], in_=kv_rows[0])
+        load_kv(0)
         for piece in range(1, PIECES):
             load_wo(piece)
-        for w in range(1, WIDTH):
-            nc.sync.dma_start(out=g_raw[w][:], in_=g_rows[w])
-            nc.sync.dma_start(out=kv_raw[w][:], in_=kv_rows[w])
+        load_g(1)
+        load_kv(1)
 
         ident_f32 = keep.tile([P, P], F32, name="ident_f32")
         make_identity(nc, ident_f32[:])
@@ -99,9 +108,9 @@ def tile_linear_retention_pb_kernel(tc, ret_w, kv_h, Wo, bo, grad_out, out):
 
         def transpose_chunk(w):
             grouped = chunk_pool.tile([P, PASSES, HEIGHT * PACK], BF16, name="g_grouped", align_bytes=64)
-            for s in range(PASSES):
-                words = grouped[:, s, :].bitcast(F32).rearrange("p (r u) -> p r u", u=HALVES)
-                for bank in range(H_BLOCKS // BANK_BLOCKS):
+            for bank in range(BANKS):
+                for s in range(PASSES):
+                    words = grouped[:, s, :].bitcast(F32).rearrange("p (r u) -> p r u", u=HALVES)
                     xt = psum_t.tile([P, HALVES, BANK_BLOCKS * P], F32, name="xt", tag="t")
                     for u in range(HALVES):
                         first = (s * HALVES + u) * P
@@ -162,14 +171,14 @@ def tile_linear_retention_pb_kernel(tc, ret_w, kv_h, Wo, bo, grad_out, out):
                     start=True,
                     stop=True,
                 )
-            out_sb = stream.tile([P, H_BLOCKS, D], F32, name="out_sb")
+            out_sb = out_pool.tile([P, H_BLOCKS, D], F32, name="out_sb")
             nc.vector.tensor_copy(out=out_sb[:], in_=out_ps[:])
             nc.sync.dma_start(out=out_rows[w, :, :, n, :], in_=out_sb[:])
 
         steps = [(w, n) for w in range(WIDTH) for n in range(HEADS)]
         transpose_chunk(0)
-        prepare_wo(0)
         finish_chunk(0)
+        prepare_wo(0)
         go_next = project(0, 0)
         for piece in range(1, PIECES_AHEAD):
             prepare_wo(piece)
@@ -185,3 +194,6 @@ def tile_linear_retention_pb_kernel(tc, ret_w, kv_h, Wo, bo, grad_out, out):
                 prepare_wo(n // PIECE_HEADS + PIECES_AHEAD)
             if n == PREPARE_AT_HEAD and w + 1 < WIDTH:
                 transpose_chunk(w + 1)
+            if n == HEADS - 1 and w + 2 < WIDTH:
+                load_g(w + 2)
+                load_kv(w + 2)

@@ -30,6 +30,8 @@ GO_PARTS = 2
 BANK_BLOCKS = 2
 BANKS = H_BLOCKS // BANK_BLOCKS
 
+WARM_MATMULS = 5
+
 FLOPS = 2 * HEIGHT * WIDTH * K * HEADS * D + 2 * HEIGHT * WIDTH * HEADS * D * D
 BYTES = 2 * (WIDTH * HEADS * D * D + K * HEADS * D + HEIGHT * WIDTH * K) + 4 * HEIGHT * WIDTH * HEADS * D
 
@@ -65,21 +67,31 @@ def tile_linear_retention_pb_kernel(tc, ret_w, kv_h, Wo, bo, grad_out, out):
                         in_=wo_rows[s, u, :, :, cols],
                     )
 
+        def load_g_bank(w, bank):
+            blocks = slice(bank * BANK_BLOCKS, (bank + 1) * BANK_BLOCKS)
+            nc.sync.dma_start(out=g_raw[w][:, blocks, :], in_=g_rows[w, :, blocks, :])
+
         def load_g(w):
             for bank in range(BANKS):
-                blocks = slice(bank * BANK_BLOCKS, (bank + 1) * BANK_BLOCKS)
-                nc.sync.dma_start(out=g_raw[w][:, blocks, :], in_=g_rows[w, :, blocks, :])
+                load_g_bank(w, bank)
 
         def load_kv(w):
             nc.sync.dma_start(out=kv_raw[w][:], in_=kv_rows[w])
 
-        load_g(0)
+        load_g_bank(0, 0)
         load_wo(0)
+        load_g_bank(0, 1)
         load_kv(0)
         for piece in range(1, PIECES):
             load_wo(piece)
         load_g(1)
         load_kv(1)
+
+        warm_sb = keep.tile([P, HEIGHT], BF16, name="warm_sb")
+        nc.vector.memset(warm_sb[:], 0.0)
+        warm_ps = psum_out.tile([P, HEIGHT], F32, name="out_ps")
+        for i in range(WARM_MATMULS):
+            nc.tensor.matmul(out=warm_ps[:], lhsT=warm_sb[:, :P], rhs=warm_sb[:], start=True, stop=True)
 
         ident_f32 = keep.tile([P, P], F32, name="ident_f32")
         make_identity(nc, ident_f32[:])
@@ -176,9 +188,9 @@ def tile_linear_retention_pb_kernel(tc, ret_w, kv_h, Wo, bo, grad_out, out):
             nc.sync.dma_start(out=out_rows[w, :, :, n, :], in_=out_sb[:])
 
         steps = [(w, n) for w in range(WIDTH) for n in range(HEADS)]
+        prepare_wo(0)
         transpose_chunk(0)
         finish_chunk(0)
-        prepare_wo(0)
         go_next = project(0, 0)
         for piece in range(1, PIECES_AHEAD):
             prepare_wo(piece)

@@ -30,6 +30,8 @@ GO_PARTS = 2
 BANK_BLOCKS = 2
 BANKS = H_BLOCKS // BANK_BLOCKS
 
+VECTOR_CHUNKS = (2, 3)
+RUN = 64
 WARM_MATMULS = 5
 
 FLOPS = 2 * HEIGHT * WIDTH * K * HEADS * D + 2 * HEIGHT * WIDTH * HEADS * D * D
@@ -40,6 +42,7 @@ def tile_linear_retention_pb_kernel(tc, ret_w, kv_h, Wo, bo, grad_out, out):
     nc = tc.nc
 
     g_rows = grad_out[0].rearrange("(hb p w) k -> w p hb k", hb=H_BLOCKS, p=P, w=WIDTH)
+    g_runs = grad_out[0].rearrange("(b r w) k -> w r b k", b=HEIGHT // 16, r=16, w=WIDTH)
     kv_rows = kv_h[0].rearrange("w n e f -> w e n f")
     wo_rows = Wo.rearrange("(s u p e) c -> s u p e c", s=PASSES, u=HALVES, p=P, e=PAIR)
     out_rows = out[0].rearrange("(hb p) w n e -> w p hb n e", hb=H_BLOCKS, p=P)
@@ -54,7 +57,13 @@ def tile_linear_retention_pb_kernel(tc, ret_w, kv_h, Wo, bo, grad_out, out):
         psum_out = ctx.enter_context(tc.psum_pool(name="psum_out", bufs=2))
         psum_t = ctx.enter_context(tc.psum_pool(name="psum_t", bufs=4))
 
-        g_raw = [keep.tile([P, H_BLOCKS, K], BF16, name="g_raw%d" % w) for w in range(WIDTH)]
+        g_raw = {}
+        x_t = {}
+        for w in range(WIDTH):
+            if w in VECTOR_CHUNKS:
+                x_t[w] = keep.tile([P, PASSES, HEIGHT * PACK], BF16, name="x_t%d" % w, align_bytes=64)
+            else:
+                g_raw[w] = keep.tile([P, H_BLOCKS, K], BF16, name="g_raw%d" % w)
         kv_raw = [keep.tile([P, HEADS, D], BF16, name="kv_raw%d" % w) for w in range(WIDTH)]
         wo_raw = [keep.tile([P, PASSES, PACK, PIECE_COLS], BF16, name="wo_raw%d" % i) for i in range(PIECES)]
 
@@ -74,6 +83,14 @@ def tile_linear_retention_pb_kernel(tc, ret_w, kv_h, Wo, bo, grad_out, out):
         def load_g(w):
             for bank in range(BANKS):
                 load_g_bank(w, bank)
+
+        def load_runs(w, s, a):
+            for u in range(HALVES):
+                first = s * K_PASS + u * PAIR * P + a * RUN
+                nc.sync.dma_start(
+                    out=x_t[w][32 * a + u : 32 * (a + 1) : HALVES, s, :].rearrange("p (b k) -> p b k", k=RUN),
+                    in_=g_runs[w, :, :, first : first + RUN],
+                )
 
         def load_kv(w):
             nc.sync.dma_start(out=kv_raw[w][:], in_=kv_rows[w])
@@ -115,12 +132,15 @@ def tile_linear_retention_pb_kernel(tc, ret_w, kv_h, Wo, bo, grad_out, out):
                     in_=grouped[:, s, :, :].rearrange("p c t -> p (c t)"),
                 )
 
+        g_grouped = {}
         transposed = {}
         chunk = {}
 
         def transpose_chunk(w):
-            grouped = chunk_pool.tile([P, PASSES, HEIGHT * PACK], BF16, name="g_grouped", align_bytes=64)
-            for bank in range(BANKS):
+            if w not in g_grouped:
+                g_grouped[w] = chunk_pool.tile([P, PASSES, HEIGHT * PACK], BF16, name="g_grouped", align_bytes=64)
+            grouped = g_grouped[w]
+            for bank in range(BANKS if w not in VECTOR_CHUNKS else 0):
                 for s in range(PASSES):
                     words = grouped[:, s, :].bitcast(F32).rearrange("p (r u) -> p r u", u=HALVES)
                     xt = psum_t.tile([P, HALVES, BANK_BLOCKS * P], F32, name="xt", tag="t")
@@ -138,6 +158,12 @@ def tile_linear_retention_pb_kernel(tc, ret_w, kv_h, Wo, bo, grad_out, out):
             for n in range(HEADS):
                 nc.tensor.transpose(kt[:, n, :], kv_raw[w][:, n, :], ident_bf16[:])
             transposed[w] = (grouped, kt)
+
+        def vector_transpose(w, s, half):
+            if w not in g_grouped:
+                g_grouped[w] = chunk_pool.tile([P, PASSES, HEIGHT * PACK], BF16, name="g_grouped", align_bytes=64)
+            cols = slice(half * HEIGHT * PACK // 2, (half + 1) * HEIGHT * PACK // 2)
+            nc.vector.transpose(out=g_grouped[w][:, s, cols].bitcast(F32), in_=x_t[w][:, s, cols].bitcast(F32))
 
         def finish_chunk(w):
             grouped, kt = transposed[w]
@@ -187,6 +213,21 @@ def tile_linear_retention_pb_kernel(tc, ret_w, kv_h, Wo, bo, grad_out, out):
             nc.vector.tensor_copy(out=out_sb[:], in_=out_ps[:])
             nc.sync.dma_start(out=out_rows[w, :, :, n, :], in_=out_sb[:])
 
+        def read_out_last(w, n, go_sb):
+            kv_t = chunk[w][2]
+            for hb in range(H_BLOCKS):
+                out_ps = psum_t.tile([P, D], F32, name="out_ps_block", tag="t")
+                nc.tensor.matmul(
+                    out=out_ps[:], lhsT=go_sb[:, hb * P : (hb + 1) * P], rhs=kv_t[:, n, :], start=True, stop=True
+                )
+                out_sb = out_pool.tile([P, D], F32, name="out_sb_block")
+                if hb % 2 == 0:
+                    nc.scalar.copy(out=out_sb[:], in_=out_ps[:])
+                    nc.scalar.dma_start(out=out_rows[w, :, hb, n, :], in_=out_sb[:])
+                else:
+                    nc.vector.tensor_copy(out=out_sb[:], in_=out_ps[:])
+                    nc.sync.dma_start(out=out_rows[w, :, hb, n, :], in_=out_sb[:])
+
         steps = [(w, n) for w in range(WIDTH) for n in range(HEADS)]
         prepare_wo(0)
         transpose_chunk(0)
@@ -201,11 +242,19 @@ def tile_linear_retention_pb_kernel(tc, ret_w, kv_h, Wo, bo, grad_out, out):
                 go_next = project(steps[i + 1][0], steps[i + 1][1])
             if n == PREPARE_AT_HEAD + 1 and w + 1 < WIDTH:
                 finish_chunk(w + 1)
-            read_out(w, n, go_now)
+            if i + 1 < len(steps):
+                read_out(w, n, go_now)
+            else:
+                read_out_last(w, n, go_now)
             if w == 0 and n % PIECE_HEADS == 0 and n // PIECE_HEADS + PIECES_AHEAD < PIECES:
                 prepare_wo(n // PIECE_HEADS + PIECES_AHEAD)
             if n == PREPARE_AT_HEAD and w + 1 < WIDTH:
                 transpose_chunk(w + 1)
+            if w + 2 in VECTOR_CHUNKS:
+                load_runs(w + 2, n // 4, n % 4)
+            if w + 1 in VECTOR_CHUNKS and n < PREPARE_AT_HEAD:
+                vector_transpose(w + 1, n // 2, n % 2)
             if n == HEADS - 1 and w + 2 < WIDTH:
-                load_g(w + 2)
+                if w + 2 not in VECTOR_CHUNKS:
+                    load_g(w + 2)
                 load_kv(w + 2)

@@ -52,7 +52,7 @@ def tile_linear_retention_pb_kernel(tc, ret_w, kv_h, Wo, bo, grad_out, out):
         keep = ctx.enter_context(tc.tile_pool(name="keep", bufs=1))
         chunk_pool = ctx.enter_context(tc.tile_pool(name="chunk", bufs=2))
         stream = ctx.enter_context(tc.tile_pool(name="stream", bufs=4))
-        out_pool = ctx.enter_context(tc.tile_pool(name="out", bufs=8))
+        out_pool = ctx.enter_context(tc.tile_pool(name="out", bufs=14))
         psum_go = ctx.enter_context(tc.psum_pool(name="psum_go", bufs=2))
         psum_out = ctx.enter_context(tc.psum_pool(name="psum_out", bufs=2))
         psum_t = ctx.enter_context(tc.psum_pool(name="psum_t", bufs=4))
@@ -103,6 +103,10 @@ def tile_linear_retention_pb_kernel(tc, ret_w, kv_h, Wo, bo, grad_out, out):
             load_wo(piece)
         load_g(1)
         load_kv(1)
+        load_kv(VECTOR_CHUNKS[0])
+        for s in range(PASSES):
+            for a in range(P // 32):
+                load_runs(VECTOR_CHUNKS[0], s, a)
 
         warm_sb = keep.tile([P, HEIGHT], BF16, name="warm_sb")
         nc.vector.memset(warm_sb[:], 0.0)
@@ -250,11 +254,12 @@ def tile_linear_retention_pb_kernel(tc, ret_w, kv_h, Wo, bo, grad_out, out):
                 prepare_wo(n // PIECE_HEADS + PIECES_AHEAD)
             if n == PREPARE_AT_HEAD and w + 1 < WIDTH:
                 transpose_chunk(w + 1)
-            if w + 2 in VECTOR_CHUNKS:
+            if w + 2 in VECTOR_CHUNKS[1:]:
+                if n == 0:
+                    load_kv(w + 2)
                 load_runs(w + 2, n // 4, n % 4)
             if w + 1 in VECTOR_CHUNKS and n < PREPARE_AT_HEAD:
                 vector_transpose(w + 1, n // 2, n % 2)
-            if n == HEADS - 1 and w + 2 < WIDTH:
-                if w + 2 not in VECTOR_CHUNKS:
-                    load_g(w + 2)
+            if n == HEADS - 1 and w + 2 < WIDTH and w + 2 not in VECTOR_CHUNKS:
+                load_g(w + 2)
                 load_kv(w + 2)

@@ -52,7 +52,7 @@ def tile_linear_retention_pb_kernel(tc, ret_w, kv_h, Wo, bo, grad_out, out):
         keep = ctx.enter_context(tc.tile_pool(name="keep", bufs=1))
         chunk_pool = ctx.enter_context(tc.tile_pool(name="chunk", bufs=2))
         stream = ctx.enter_context(tc.tile_pool(name="stream", bufs=4))
-        out_pool = ctx.enter_context(tc.tile_pool(name="out", bufs=14))
+        out_pool = ctx.enter_context(tc.tile_pool(name="out", bufs=20))
         psum_go = ctx.enter_context(tc.psum_pool(name="psum_go", bufs=2))
         psum_out = ctx.enter_context(tc.psum_pool(name="psum_out", bufs=2))
         psum_t = ctx.enter_context(tc.psum_pool(name="psum_t", bufs=4))
@@ -103,10 +103,11 @@ def tile_linear_retention_pb_kernel(tc, ret_w, kv_h, Wo, bo, grad_out, out):
             load_wo(piece)
         load_g(1)
         load_kv(1)
-        load_kv(VECTOR_CHUNKS[0])
-        for s in range(PASSES):
-            for a in range(P // 32):
-                load_runs(VECTOR_CHUNKS[0], s, a)
+        for w in VECTOR_CHUNKS:
+            load_kv(w)
+            for s in range(PASSES):
+                for a in range(P // 32):
+                    load_runs(w, s, a)
 
         warm_sb = keep.tile([P, HEIGHT], BF16, name="warm_sb")
         nc.vector.memset(warm_sb[:], 0.0)
@@ -254,10 +255,6 @@ def tile_linear_retention_pb_kernel(tc, ret_w, kv_h, Wo, bo, grad_out, out):
                 prepare_wo(n // PIECE_HEADS + PIECES_AHEAD)
             if n == PREPARE_AT_HEAD and w + 1 < WIDTH:
                 transpose_chunk(w + 1)
-            if w + 2 in VECTOR_CHUNKS[1:]:
-                if n == 0:
-                    load_kv(w + 2)
-                load_runs(w + 2, n // 4, n % 4)
             if w + 1 in VECTOR_CHUNKS and n < PREPARE_AT_HEAD:
                 vector_transpose(w + 1, n // 2, n % 2)
             if n == HEADS - 1 and w + 2 < WIDTH and w + 2 not in VECTOR_CHUNKS:

@@ -32,6 +32,8 @@ BANKS = H_BLOCKS // BANK_BLOCKS
 
 VECTOR_CHUNKS = (2, 3)
 RUN = 64
+STORE_GROUPS = (4, 4)
+LAST_STORE_GROUPS = (4, 2, 1)
 WARM_MATMULS = 5
 
 FLOPS = 2 * HEIGHT * WIDTH * K * HEADS * D + 2 * HEIGHT * WIDTH * HEADS * D * D
@@ -43,6 +45,7 @@ def tile_linear_retention_pb_kernel(tc, ret_w, kv_h, Wo, bo, grad_out, out):
 
     g_rows = grad_out[0].rearrange("(hb p w) k -> w p hb k", hb=H_BLOCKS, p=P, w=WIDTH)
     g_runs = grad_out[0].rearrange("(b r w) k -> w r b k", b=HEIGHT // 16, r=16, w=WIDTH)
+    kv_runs = kv_h[0].rearrange("w n (eh j) (a i) -> w a j (n eh) i", eh=D // 32, j=32, a=D // 32, i=32)
     kv_rows = kv_h[0].rearrange("w n e f -> w e n f")
     wo_rows = Wo.rearrange("(s u p e) c -> s u p e c", s=PASSES, u=HALVES, p=P, e=PAIR)
     out_rows = out[0].rearrange("(hb p) w n e -> w p hb n e", hb=H_BLOCKS, p=P)
@@ -52,10 +55,9 @@ def tile_linear_retention_pb_kernel(tc, ret_w, kv_h, Wo, bo, grad_out, out):
         keep = ctx.enter_context(tc.tile_pool(name="keep", bufs=1))
         chunk_pool = ctx.enter_context(tc.tile_pool(name="chunk", bufs=2))
         stream = ctx.enter_context(tc.tile_pool(name="stream", bufs=4))
-        out_pool = ctx.enter_context(tc.tile_pool(name="out", bufs=20))
+        out_pool = ctx.enter_context(tc.tile_pool(name="out", bufs=7))
         psum_go = ctx.enter_context(tc.psum_pool(name="psum_go", bufs=2))
-        psum_out = ctx.enter_context(tc.psum_pool(name="psum_out", bufs=2))
-        psum_t = ctx.enter_context(tc.psum_pool(name="psum_t", bufs=4))
+        psum_t = ctx.enter_context(tc.psum_pool(name="psum_t", bufs=6))
 
         g_raw = {}
         x_t = {}
@@ -64,7 +66,7 @@ def tile_linear_retention_pb_kernel(tc, ret_w, kv_h, Wo, bo, grad_out, out):
                 x_t[w] = keep.tile([P, PASSES, HEIGHT * PACK], BF16, name="x_t%d" % w, align_bytes=64)
             else:
                 g_raw[w] = keep.tile([P, H_BLOCKS, K], BF16, name="g_raw%d" % w)
-        kv_raw = [keep.tile([P, HEADS, D], BF16, name="kv_raw%d" % w) for w in range(WIDTH)]
+        kv_raw = [keep.tile([P, HEADS, D], BF16, name="kv_raw%d" % w, align_bytes=64) for w in range(WIDTH)]
         wo_raw = [keep.tile([P, PASSES, PACK, PIECE_COLS], BF16, name="wo_raw%d" % i) for i in range(PIECES)]
 
         def load_wo(piece):
@@ -95,6 +97,13 @@ def tile_linear_retention_pb_kernel(tc, ret_w, kv_h, Wo, bo, grad_out, out):
         def load_kv(w):
             nc.sync.dma_start(out=kv_raw[w][:], in_=kv_rows[w])
 
+        def load_kv_runs(w):
+            for a in range(P // 32):
+                nc.sync.dma_start(
+                    out=kv_raw[w][32 * a : 32 * (a + 1), :, :].rearrange("p n (eh i) -> p (n eh) i", i=32),
+                    in_=kv_runs[w, a],
+                )
+
         load_g_bank(0, 0)
         load_wo(0)
         load_g_bank(0, 1)
@@ -104,14 +113,14 @@ def tile_linear_retention_pb_kernel(tc, ret_w, kv_h, Wo, bo, grad_out, out):
         load_g(1)
         load_kv(1)
         for w in VECTOR_CHUNKS:
-            load_kv(w)
             for s in range(PASSES):
                 for a in range(P // 32):
                     load_runs(w, s, a)
+            load_kv_runs(w)
 
         warm_sb = keep.tile([P, HEIGHT], BF16, name="warm_sb")
         nc.vector.memset(warm_sb[:], 0.0)
-        warm_ps = psum_out.tile([P, HEIGHT], F32, name="out_ps")
+        warm_ps = psum_t.tile([P, HEIGHT], F32, name="warm_ps", tag="t")
         for i in range(WARM_MATMULS):
             nc.tensor.matmul(out=warm_ps[:], lhsT=warm_sb[:, :P], rhs=warm_sb[:], start=True, stop=True)
 
@@ -145,7 +154,7 @@ def tile_linear_retention_pb_kernel(tc, ret_w, kv_h, Wo, bo, grad_out, out):
             if w not in g_grouped:
                 g_grouped[w] = chunk_pool.tile([P, PASSES, HEIGHT * PACK], BF16, name="g_grouped", align_bytes=64)
             grouped = g_grouped[w]
-            for bank in range(BANKS if w not in VECTOR_CHUNKS else 0):
+            for bank in range(BANKS):
                 for s in range(PASSES):
                     words = grouped[:, s, :].bitcast(F32).rearrange("p (r u) -> p r u", u=HALVES)
                     xt = psum_t.tile([P, HALVES, BANK_BLOCKS * P], F32, name="xt", tag="t")
@@ -169,6 +178,13 @@ def tile_linear_retention_pb_kernel(tc, ret_w, kv_h, Wo, bo, grad_out, out):
                 g_grouped[w] = chunk_pool.tile([P, PASSES, HEIGHT * PACK], BF16, name="g_grouped", align_bytes=64)
             cols = slice(half * HEIGHT * PACK // 2, (half + 1) * HEIGHT * PACK // 2)
             nc.vector.transpose(out=g_grouped[w][:, s, cols].bitcast(F32), in_=x_t[w][:, s, cols].bitcast(F32))
+
+        def vector_transpose_kv(w):
+            kt = chunk_pool.tile([P, HEADS, D], BF16, name="kt_sb", align_bytes=64)
+            nc.vector.transpose(
+                out=kt[:].rearrange("p n e -> p (n e)"), in_=kv_raw[w][:].rearrange("p n e -> p (n e)")
+            )
+            transposed[w] = (g_grouped[w], kt)
 
         def finish_chunk(w):
             grouped, kt = transposed[w]
@@ -203,9 +219,11 @@ def tile_linear_retention_pb_kernel(tc, ret_w, kv_h, Wo, bo, grad_out, out):
                 nc.scalar.copy(out=go_sb[:, tokens], in_=go_ps[:, tokens])
             return go_sb
 
+        store_tiles = {}
+
         def read_out(w, n, go_sb):
             kv_t = chunk[w][2]
-            out_ps = psum_out.tile([P, H_BLOCKS, D], F32, name="out_ps")
+            out_ps = psum_t.tile([P, H_BLOCKS, D], F32, name="out_ps", tag="t")
             for hb in range(H_BLOCKS):
                 nc.tensor.matmul(
                     out=out_ps[:, hb, :],
@@ -214,9 +232,15 @@ def tile_linear_retention_pb_kernel(tc, ret_w, kv_h, Wo, bo, grad_out, out):
                     start=True,
                     stop=True,
                 )
-            out_sb = out_pool.tile([P, H_BLOCKS, D], F32, name="out_sb")
-            nc.vector.tensor_copy(out=out_sb[:], in_=out_ps[:])
-            nc.sync.dma_start(out=out_rows[w, :, :, n, :], in_=out_sb[:])
+            first = 0
+            for size in (LAST_STORE_GROUPS if w == WIDTH - 1 else STORE_GROUPS):
+                if first <= n < first + size:
+                    if n == first:
+                        store_tiles[w] = out_pool.tile([P, H_BLOCKS, size, D], F32, name="out_sb")
+                    nc.vector.tensor_copy(out=store_tiles[w][:, :, n - first, :], in_=out_ps[:])
+                    if n == first + size - 1:
+                        nc.sync.dma_start(out=out_rows[w, :, :, first : first + size, :], in_=store_tiles[w][:])
+                first += size
 
         def read_out_last(w, n, go_sb):
             kv_t = chunk[w][2]
@@ -254,7 +278,10 @@ def tile_linear_retention_pb_kernel(tc, ret_w, kv_h, Wo, bo, grad_out, out):
             if w == 0 and n % PIECE_HEADS == 0 and n // PIECE_HEADS + PIECES_AHEAD < PIECES:
                 prepare_wo(n // PIECE_HEADS + PIECES_AHEAD)
             if n == PREPARE_AT_HEAD and w + 1 < WIDTH:
-                transpose_chunk(w + 1)
+                if w + 1 in VECTOR_CHUNKS:
+                    vector_transpose_kv(w + 1)
+                else:
+                    transpose_chunk(w + 1)
             if w + 1 in VECTOR_CHUNKS and n < PREPARE_AT_HEAD:
                 vector_transpose(w + 1, n // 2, n % 2)
             if n == HEADS - 1 and w + 2 < WIDTH and w + 2 not in VECTOR_CHUNKS:

@@ -30,10 +30,12 @@ GO_PARTS = 2
 BANK_BLOCKS = 2
 BANKS = H_BLOCKS // BANK_BLOCKS
 
+KV_VECTOR_CHUNKS = (2, 3)
 VECTOR_CHUNKS = (2, 3)
 RUN = 64
 STORE_GROUPS = (4, 4)
 LAST_STORE_GROUPS = (4, 2, 1)
+E_LOW = 8
 WARM_MATMULS = 5
 
 FLOPS = 2 * HEIGHT * WIDTH * K * HEADS * D + 2 * HEIGHT * WIDTH * HEADS * D * D
@@ -46,7 +48,7 @@ def tile_linear_retention_pb_kernel(tc, ret_w, kv_h, Wo, bo, grad_out, out):
     g_rows = grad_out[0].rearrange("(hb p w) k -> w p hb k", hb=H_BLOCKS, p=P, w=WIDTH)
     g_runs = grad_out[0].rearrange("(b r w) k -> w r b k", b=HEIGHT // 16, r=16, w=WIDTH)
     kv_runs = kv_h[0].rearrange("w n (eh j) (a i) -> w a j (n eh) i", eh=D // 32, j=32, a=D // 32, i=32)
-    kv_rows = kv_h[0].rearrange("w n e f -> w e n f")
+    kv_rows = kv_h[0].rearrange("w n (eh el) f -> w (n eh) (el f)", el=E_LOW)
     wo_rows = Wo.rearrange("(s u p e) c -> s u p e c", s=PASSES, u=HALVES, p=P, e=PAIR)
     out_rows = out[0].rearrange("(hb p) w n e -> w p hb n e", hb=H_BLOCKS, p=P)
 
@@ -67,24 +69,19 @@ def tile_linear_retention_pb_kernel(tc, ret_w, kv_h, Wo, bo, grad_out, out):
             else:
                 g_raw[w] = keep.tile([P, H_BLOCKS, K], BF16, name="g_raw%d" % w)
         kv_raw = [keep.tile([P, HEADS, D], BF16, name="kv_raw%d" % w, align_bytes=64) for w in range(WIDTH)]
-        wo_raw = [keep.tile([P, PASSES, PACK, PIECE_COLS], BF16, name="wo_raw%d" % i) for i in range(PIECES)]
+        wo_raw = [keep.tile([P, PACK, PASSES, PIECE_COLS], BF16, name="wo_raw%d" % i) for i in range(PIECES)]
 
-        def load_wo(piece):
+        def load_wo(piece, s):
             cols = slice(piece * PIECE_COLS, (piece + 1) * PIECE_COLS)
-            for s in range(PASSES):
-                for u in range(HALVES):
-                    nc.sync.dma_start(
-                        out=wo_raw[piece][:, s, PAIR * u : PAIR * (u + 1), :],
-                        in_=wo_rows[s, u, :, :, cols],
-                    )
+            for u in range(HALVES):
+                nc.sync.dma_start(
+                    out=wo_raw[piece][:, PAIR * u : PAIR * (u + 1), s, :],
+                    in_=wo_rows[s, u, :, :, cols],
+                )
 
         def load_g_bank(w, bank):
             blocks = slice(bank * BANK_BLOCKS, (bank + 1) * BANK_BLOCKS)
             nc.sync.dma_start(out=g_raw[w][:, blocks, :], in_=g_rows[w, :, blocks, :])
-
-        def load_g(w):
-            for bank in range(BANKS):
-                load_g_bank(w, bank)
 
         def load_runs(w, s, a):
             for u in range(HALVES):
@@ -95,7 +92,7 @@ def tile_linear_retention_pb_kernel(tc, ret_w, kv_h, Wo, bo, grad_out, out):
                 )
 
         def load_kv(w):
-            nc.sync.dma_start(out=kv_raw[w][:], in_=kv_rows[w])
+            nc.sync.dma_start(out=kv_raw[w][:].rearrange("p el f -> p (el f)"), in_=kv_rows[w])
 
         def load_kv_runs(w):
             for a in range(P // 32):
@@ -105,18 +102,23 @@ def tile_linear_retention_pb_kernel(tc, ret_w, kv_h, Wo, bo, grad_out, out):
                 )
 
         load_g_bank(0, 0)
-        load_wo(0)
+        for s in range(PASSES):
+            load_wo(0, s)
         load_g_bank(0, 1)
-        load_kv(0)
+        for w in range(WIDTH):
+            if w not in KV_VECTOR_CHUNKS:
+                load_kv(w)
         for piece in range(1, PIECES):
-            load_wo(piece)
-        load_g(1)
-        load_kv(1)
+            for s in range(PASSES):
+                load_wo(piece, s)
+        for bank in range(BANKS):
+            load_g_bank(1, bank)
         for w in VECTOR_CHUNKS:
             for s in range(PASSES):
                 for a in range(P // 32):
                     load_runs(w, s, a)
-            load_kv_runs(w)
+            if w in KV_VECTOR_CHUNKS:
+                load_kv_runs(w)
 
         warm_sb = keep.tile([P, HEIGHT], BF16, name="warm_sb")
         nc.vector.memset(warm_sb[:], 0.0)
@@ -133,45 +135,43 @@ def tile_linear_retention_pb_kernel(tc, ret_w, kv_h, Wo, bo, grad_out, out):
         wo_scales = [keep.tile([P, PASSES, PIECE_COLS], U8, name="wo_scales%d" % i, align_bytes=64) for i in range(PIECES)]
 
         def prepare_wo(piece):
-            grouped = chunk_pool.tile([P, PASSES, PIECE_COLS, PACK], BF16, name="wo_grouped", align_bytes=64)
-            for s in range(PASSES):
-                nc.vector.tensor_copy(
-                    out=grouped[:, s, :, :].rearrange("p (c i) t -> p c t i", i=4),
-                    in_=wo_raw[piece][:, s, :, :].rearrange("p t (c i) -> p c t i", i=4),
-                )
-            for s in range(PASSES):
-                nc.vector.quantize_mx(
-                    out=wo_codes[piece][:, s, :].bitcast(E4M3_X4),
-                    scales=wo_scales[piece][:, s, :],
-                    in_=grouped[:, s, :, :].rearrange("p c t -> p (c t)"),
-                )
+            grouped = chunk_pool.tile([P, PASSES * PIECE_COLS, PACK], BF16, name="wo_grouped", align_bytes=64)
+            nc.vector.tensor_copy(
+                out=grouped[:].rearrange("p (c i) t -> p c t i", i=4),
+                in_=wo_raw[piece][:].rearrange("p t s (c i) -> p (s c) t i", i=4),
+            )
+            nc.vector.quantize_mx(
+                out=wo_codes[piece][:].rearrange("p s c -> p (s c)").bitcast(E4M3_X4),
+                scales=wo_scales[piece][:].rearrange("p s c -> p (s c)"),
+                in_=grouped[:].rearrange("p c t -> p (c t)"),
+            )
 
         g_grouped = {}
-        transposed = {}
+        kv_wide = {}
+        kv_turned = {}
         chunk = {}
 
-        def transpose_chunk(w):
+        def transpose_g(w, bank, s):
             if w not in g_grouped:
                 g_grouped[w] = chunk_pool.tile([P, PASSES, HEIGHT * PACK], BF16, name="g_grouped", align_bytes=64)
-            grouped = g_grouped[w]
-            for bank in range(BANKS):
-                for s in range(PASSES):
-                    words = grouped[:, s, :].bitcast(F32).rearrange("p (r u) -> p r u", u=HALVES)
-                    xt = psum_t.tile([P, HALVES, BANK_BLOCKS * P], F32, name="xt", tag="t")
-                    for u in range(HALVES):
-                        first = (s * HALVES + u) * P
-                        for b in range(BANK_BLOCKS):
-                            nc.tensor.transpose(
-                                xt[:, u, b * P : (b + 1) * P],
-                                g_raw[w][:, bank * BANK_BLOCKS + b, :].bitcast(F32)[:, first : first + P],
-                                ident_f32[:],
-                            )
-                    tokens = slice(bank * BANK_BLOCKS * P, (bank + 1) * BANK_BLOCKS * P)
-                    nc.scalar.copy(out=words[:, tokens, :], in_=xt[:].rearrange("p u r -> p r u"))
-            kt = psum_t.tile([P, HEADS, D], BF16, name="kt", tag="t")
-            for n in range(HEADS):
-                nc.tensor.transpose(kt[:, n, :], kv_raw[w][:, n, :], ident_bf16[:])
-            transposed[w] = (grouped, kt)
+            words = g_grouped[w][:, s, :].bitcast(F32).rearrange("p (r u) -> p r u", u=HALVES)
+            xt = psum_t.tile([P, HALVES, BANK_BLOCKS * P], F32, name="xt", tag="t")
+            for u in range(HALVES):
+                first = (s * HALVES + u) * P
+                for b in range(BANK_BLOCKS):
+                    nc.tensor.transpose(
+                        xt[:, u, b * P : (b + 1) * P],
+                        g_raw[w][:, bank * BANK_BLOCKS + b, :].bitcast(F32)[:, first : first + P],
+                        ident_f32[:],
+                    )
+            tokens = slice(bank * BANK_BLOCKS * P, (bank + 1) * BANK_BLOCKS * P)
+            nc.scalar.copy(out=words[:, tokens, :], in_=xt[:].rearrange("p u r -> p r u"))
+
+        def transpose_kv(w):
+            kt = psum_t.tile([P, E_LOW, P], BF16, name="kt", tag="t")
+            for el in range(E_LOW):
+                nc.tensor.transpose(kt[:, el, :], kv_raw[w][:, el, :], ident_bf16[:])
+            kv_turned[w] = kt
 
         def vector_transpose(w, s, half):
             if w not in g_grouped:
@@ -184,45 +184,58 @@ def tile_linear_retention_pb_kernel(tc, ret_w, kv_h, Wo, bo, grad_out, out):
             nc.vector.transpose(
                 out=kt[:].rearrange("p n e -> p (n e)"), in_=kv_raw[w][:].rearrange("p n e -> p (n e)")
             )
-            transposed[w] = (g_grouped[w], kt)
+            kv_turned[w] = kt
 
-        def finish_chunk(w):
-            grouped, kt = transposed[w]
+        def quantise_g(w, s):
+            if w not in chunk:
+                codes = chunk_pool.tile([P, PASSES, HEIGHT], U32, name="g_codes", align_bytes=64)
+                scales = chunk_pool.tile([P, PASSES, HEIGHT], U8, name="g_scales", align_bytes=64)
+                chunk[w] = [codes, scales, None]
+            nc.vector.quantize_mx(
+                out=chunk[w][0][:, s, :].bitcast(E5M2_X4), scales=chunk[w][1][:, s, :], in_=g_grouped[w][:, s, :]
+            )
+
+        def widen_kv(w):
             kv_t = chunk_pool.tile([P, HEADS, D], F32, name="kv_t")
-            nc.scalar.copy(out=kv_t[:], in_=kt[:])
-            codes = chunk_pool.tile([P, PASSES, HEIGHT], U32, name="g_codes", align_bytes=64)
-            scales = chunk_pool.tile([P, PASSES, HEIGHT], U8, name="g_scales", align_bytes=64)
-            for s in range(PASSES):
-                nc.vector.quantize_mx(
-                    out=codes[:, s, :].bitcast(E5M2_X4), scales=scales[:, s, :], in_=grouped[:, s, :]
+            if w in KV_VECTOR_CHUNKS:
+                nc.scalar.copy(out=kv_t[:], in_=kv_turned[w][:])
+            else:
+                nc.scalar.copy(
+                    out=kv_t[:].rearrange("p n (eh el) -> p (n eh) el", el=E_LOW),
+                    in_=kv_turned[w][:].rearrange("p el q -> p q el"),
                 )
-            chunk[w] = (codes, scales, kv_t)
+            kv_wide[w] = kv_t
 
-        def project(w, n):
-            codes, scales = chunk[w][0], chunk[w][1]
+        def mx_pass(w, n, s, go_ps):
             piece = n // PIECE_HEADS
             cols = slice((n % PIECE_HEADS) * D, (n % PIECE_HEADS + 1) * D)
-            go_ps = psum_go.tile([P, HEIGHT], F32, name="go_ps")
-            for s in range(PASSES):
-                nc.tensor.matmul_mx(
-                    out=go_ps[:],
-                    lhsT=wo_codes[piece][:, s, cols].bitcast(E4M3_X4),
-                    lhsT_scale=wo_scales[piece][:, s, cols],
-                    rhs=codes[:, s, :].bitcast(E5M2_X4),
-                    rhs_scale=scales[:, s, :],
-                    start=(s == 0),
-                    stop=(s == PASSES - 1),
-                )
+            nc.tensor.matmul_mx(
+                out=go_ps[:],
+                lhsT=wo_codes[piece][:, s, cols].bitcast(E4M3_X4),
+                lhsT_scale=wo_scales[piece][:, s, cols],
+                rhs=chunk[w][0][:, s, :].bitcast(E5M2_X4),
+                rhs_scale=chunk[w][1][:, s, :],
+                start=(s == 0),
+                stop=(s == PASSES - 1),
+            )
+
+        def copy_go(go_ps):
             go_sb = stream.tile([P, HEIGHT], F32, name="go_sb")
             for part in range(GO_PARTS):
                 tokens = slice(part * HEIGHT // GO_PARTS, (part + 1) * HEIGHT // GO_PARTS)
                 nc.scalar.copy(out=go_sb[:, tokens], in_=go_ps[:, tokens])
             return go_sb
 
+        def project(w, n):
+            go_ps = psum_go.tile([P, HEIGHT], F32, name="go_ps")
+            for s in range(PASSES):
+                mx_pass(w, n, s, go_ps)
+            return copy_go(go_ps)
+
         store_tiles = {}
 
         def read_out(w, n, go_sb):
-            kv_t = chunk[w][2]
+            kv_t = kv_wide[w]
             out_ps = psum_t.tile([P, H_BLOCKS, D], F32, name="out_ps", tag="t")
             for hb in range(H_BLOCKS):
                 nc.tensor.matmul(
@@ -243,7 +256,7 @@ def tile_linear_retention_pb_kernel(tc, ret_w, kv_h, Wo, bo, grad_out, out):
                 first += size
 
         def read_out_last(w, n, go_sb):
-            kv_t = chunk[w][2]
+            kv_t = kv_wide[w]
             for hb in range(H_BLOCKS):
                 out_ps = psum_t.tile([P, D], F32, name="out_ps_block", tag="t")
                 nc.tensor.matmul(
@@ -259,31 +272,39 @@ def tile_linear_retention_pb_kernel(tc, ret_w, kv_h, Wo, bo, grad_out, out):
 
         steps = [(w, n) for w in range(WIDTH) for n in range(HEADS)]
         prepare_wo(0)
-        transpose_chunk(0)
-        finish_chunk(0)
-        go_next = project(0, 0)
+        for bank in range(BANKS):
+            for s in range(PASSES):
+                transpose_g(0, bank, s)
+        for w in range(WIDTH):
+            if w not in KV_VECTOR_CHUNKS:
+                transpose_kv(w)
+        widen_kv(0)
+        for s in range(PASSES):
+            quantise_g(0, s)
+        go = {0: project(0, 0)}
         for piece in range(1, PIECES_AHEAD):
             prepare_wo(piece)
         for i in range(len(steps)):
             w, n = steps[i]
-            go_now = go_next
-            if i + 1 < len(steps):
-                go_next = project(steps[i + 1][0], steps[i + 1][1])
+            if i + 1 < len(steps) and i + 1 not in go:
+                go[i + 1] = project(steps[i + 1][0], steps[i + 1][1])
+            go_now = go[i]
             if n == PREPARE_AT_HEAD + 1 and w + 1 < WIDTH:
-                finish_chunk(w + 1)
+                for s in range(PASSES):
+                    quantise_g(w + 1, s)
+                widen_kv(w + 1)
             if i + 1 < len(steps):
                 read_out(w, n, go_now)
             else:
                 read_out_last(w, n, go_now)
             if w == 0 and n % PIECE_HEADS == 0 and n // PIECE_HEADS + PIECES_AHEAD < PIECES:
                 prepare_wo(n // PIECE_HEADS + PIECES_AHEAD)
-            if n == PREPARE_AT_HEAD and w + 1 < WIDTH:
-                if w + 1 in VECTOR_CHUNKS:
+            if w + 1 in KV_VECTOR_CHUNKS:
+                if n < PREPARE_AT_HEAD:
+                    vector_transpose(w + 1, n // 2, n % 2)
+                elif n == PREPARE_AT_HEAD:
                     vector_transpose_kv(w + 1)
-                else:
-                    transpose_chunk(w + 1)
-            if w + 1 in VECTOR_CHUNKS and n < PREPARE_AT_HEAD:
-                vector_transpose(w + 1, n // 2, n % 2)
-            if n == HEADS - 1 and w + 2 < WIDTH and w + 2 not in VECTOR_CHUNKS:
-                load_g(w + 2)
-                load_kv(w + 2)
+            elif w + 1 < WIDTH and n == PREPARE_AT_HEAD:
+                for bank in range(BANKS):
+                    for s in range(PASSES):
+                        transpose_g(w + 1, bank, s)

@@ -36,6 +36,7 @@ RUN = 64
 STORE_GROUPS = (4, 4)
 LAST_STORE_GROUPS = (4, 2, 1)
 E_LOW = 8
+WARM_BETWEEN_LOADS = 3
 WARM_MATMULS = 5
 
 FLOPS = 2 * HEIGHT * WIDTH * K * HEADS * D + 2 * HEIGHT * WIDTH * HEADS * D * D
@@ -123,8 +124,12 @@ def tile_linear_retention_pb_kernel(tc, ret_w, kv_h, Wo, bo, grad_out, out):
         warm_sb = keep.tile([P, HEIGHT], BF16, name="warm_sb")
         nc.vector.memset(warm_sb[:], 0.0)
         warm_ps = psum_t.tile([P, HEIGHT], F32, name="warm_ps", tag="t")
-        for i in range(WARM_MATMULS):
-            nc.tensor.matmul(out=warm_ps[:], lhsT=warm_sb[:, :P], rhs=warm_sb[:], start=True, stop=True)
+
+        def warm(count):
+            for i in range(count):
+                nc.tensor.matmul(out=warm_ps[:], lhsT=warm_sb[:, :P], rhs=warm_sb[:], start=True, stop=True)
+
+        warm(WARM_MATMULS)
 
         ident_f32 = keep.tile([P, P], F32, name="ident_f32")
         make_identity(nc, ident_f32[:])
@@ -275,9 +280,12 @@ def tile_linear_retention_pb_kernel(tc, ret_w, kv_h, Wo, bo, grad_out, out):
         for bank in range(BANKS):
             for s in range(PASSES):
                 transpose_g(0, bank, s)
+            if bank == 0:
+                warm(WARM_BETWEEN_LOADS)
         for w in range(WIDTH):
             if w not in KV_VECTOR_CHUNKS:
                 transpose_kv(w)
+                warm(1)
         widen_kv(0)
         for s in range(PASSES):
             quantise_g(0, s)

@@ -170,7 +170,8 @@ def tile_linear_retention_pb_kernel(tc, ret_w, kv_h, Wo, bo, grad_out, out):
                         ident_f32[:],
                     )
             tokens = slice(bank * BANK_BLOCKS * P, (bank + 1) * BANK_BLOCKS * P)
-            nc.scalar.copy(out=words[:, tokens, :], in_=xt[:].rearrange("p u r -> p r u"))
+            copy = nc.scalar.copy if w == 0 else nc.vector.tensor_copy
+            copy(out=words[:, tokens, :], in_=xt[:].rearrange("p u r -> p r u"))
 
         def transpose_kv(w):
             kt = psum_t.tile([P, E_LOW, P], BF16, name="kt", tag="t")
@@ -202,10 +203,11 @@ def tile_linear_retention_pb_kernel(tc, ret_w, kv_h, Wo, bo, grad_out, out):
 
         def widen_kv(w):
             kv_t = chunk_pool.tile([P, HEADS, D], F32, name="kv_t")
+            copy = nc.scalar.copy if w == 0 else nc.vector.tensor_copy
             if w in KV_VECTOR_CHUNKS:
-                nc.scalar.copy(out=kv_t[:], in_=kv_turned[w][:])
+                copy(out=kv_t[:], in_=kv_turned[w][:])
             else:
-                nc.scalar.copy(
+                copy(
                     out=kv_t[:].rearrange("p n (eh el) -> p (n eh) el", el=E_LOW),
                     in_=kv_turned[w][:].rearrange("p el q -> p q el"),
                 )
@@ -255,7 +257,7 @@ def tile_linear_retention_pb_kernel(tc, ret_w, kv_h, Wo, bo, grad_out, out):
                 if first <= n < first + size:
                     if n == first:
                         store_tiles[w] = out_pool.tile([P, H_BLOCKS, size, D], F32, name="out_sb")
-                    nc.vector.tensor_copy(out=store_tiles[w][:, :, n - first, :], in_=out_ps[:])
+                    nc.scalar.copy(out=store_tiles[w][:, :, n - first, :], in_=out_ps[:])
                     if n == first + size - 1:
                         nc.sync.dma_start(out=out_rows[w, :, :, first : first + size, :], in_=store_tiles[w][:])
                 first += size

@@ -25,13 +25,14 @@ PIECE_HEADS = 2
 PIECE_COLS = PIECE_HEADS * D
 PIECES = HEADS // PIECE_HEADS
 PIECES_AHEAD = 2
-PREPARE_AT_HEAD = 4
+PREPARE_AT_HEADS = (3, 5)
+WIDEN_AT_HEAD = 6
 GO_PARTS = 2
 BANK_BLOCKS = 2
 BANKS = H_BLOCKS // BANK_BLOCKS
 
 KV_VECTOR_CHUNKS = (2, 3)
-VECTOR_CHUNKS = (2, 3)
+VECTOR_CHUNKS = (1, 2, 3)
 RUN = 64
 STORE_GROUPS = (4, 4)
 LAST_STORE_GROUPS = (4, 2, 1)
@@ -112,8 +113,6 @@ def tile_linear_retention_pb_kernel(tc, ret_w, kv_h, Wo, bo, grad_out, out):
         for piece in range(1, PIECES):
             for s in range(PASSES):
                 load_wo(piece, s)
-        for bank in range(BANKS):
-            load_g_bank(1, bank)
         for w in VECTOR_CHUNKS:
             for s in range(PASSES):
                 for a in range(P // 32):
@@ -170,8 +169,7 @@ def tile_linear_retention_pb_kernel(tc, ret_w, kv_h, Wo, bo, grad_out, out):
                         ident_f32[:],
                     )
             tokens = slice(bank * BANK_BLOCKS * P, (bank + 1) * BANK_BLOCKS * P)
-            copy = nc.scalar.copy if w == 0 else nc.vector.tensor_copy
-            copy(out=words[:, tokens, :], in_=xt[:].rearrange("p u r -> p r u"))
+            nc.scalar.copy(out=words[:, tokens, :], in_=xt[:].rearrange("p u r -> p r u"))
 
         def transpose_kv(w):
             kt = psum_t.tile([P, E_LOW, P], BF16, name="kt", tag="t")
@@ -299,22 +297,19 @@ def tile_linear_retention_pb_kernel(tc, ret_w, kv_h, Wo, bo, grad_out, out):
             if i + 1 < len(steps) and i + 1 not in go:
                 go[i + 1] = project(steps[i + 1][0], steps[i + 1][1])
             go_now = go[i]
-            if n == PREPARE_AT_HEAD + 1 and w + 1 < WIDTH:
-                for s in range(PASSES):
-                    quantise_g(w + 1, s)
-                widen_kv(w + 1)
             if i + 1 < len(steps):
                 read_out(w, n, go_now)
             else:
                 read_out_last(w, n, go_now)
             if w == 0 and n % PIECE_HEADS == 0 and n // PIECE_HEADS + PIECES_AHEAD < PIECES:
                 prepare_wo(n // PIECE_HEADS + PIECES_AHEAD)
-            if w + 1 in KV_VECTOR_CHUNKS:
-                if n < PREPARE_AT_HEAD:
-                    vector_transpose(w + 1, n // 2, n % 2)
-                elif n == PREPARE_AT_HEAD:
-                    vector_transpose_kv(w + 1)
-            elif w + 1 < WIDTH and n == PREPARE_AT_HEAD:
-                for bank in range(BANKS):
-                    for s in range(PASSES):
-                        transpose_g(w + 1, bank, s)
+            if w + 1 < WIDTH and n in PREPARE_AT_HEADS:
+                s = PREPARE_AT_HEADS.index(n)
+                if w == 0 and s == 0:
+                    widen_kv(1)
+                for half in range(2):
+                    vector_transpose(w + 1, s, half)
+                quantise_g(w + 1, s)
+            if n == WIDEN_AT_HEAD and w + 1 in KV_VECTOR_CHUNKS:
+                vector_transpose_kv(w + 1)
+                widen_kv(w + 1)

@@ -32,6 +32,7 @@ BANK_BLOCKS = 2
 BANKS = H_BLOCKS // BANK_BLOCKS
 
 KV_VECTOR_CHUNKS = (2, 3)
+VECTOR_PASSES = {1: (1,), 2: (0, 1), 3: (0, 1)}
 VECTOR_CHUNKS = (1, 2, 3)
 RUN = 64
 STORE_GROUPS = (4, 4)
@@ -70,6 +71,8 @@ def tile_linear_retention_pb_kernel(tc, ret_w, kv_h, Wo, bo, grad_out, out):
                 x_t[w] = keep.tile([P, PASSES, HEIGHT * PACK], BF16, name="x_t%d" % w, align_bytes=64)
             else:
                 g_raw[w] = keep.tile([P, H_BLOCKS, K], BF16, name="g_raw%d" % w)
+            if w == 1:
+                g_raw[w] = keep.tile([P, H_BLOCKS, K_PASS], BF16, name="g_raw%d" % w)
         kv_raw = [keep.tile([P, HEADS, D], BF16, name="kv_raw%d" % w, align_bytes=64) for w in range(WIDTH)]
         wo_raw = [keep.tile([P, PACK, PASSES, PIECE_COLS], BF16, name="wo_raw%d" % i) for i in range(PIECES)]
 
@@ -114,7 +117,9 @@ def tile_linear_retention_pb_kernel(tc, ret_w, kv_h, Wo, bo, grad_out, out):
             for s in range(PASSES):
                 load_wo(piece, s)
         for w in VECTOR_CHUNKS:
-            for s in range(PASSES):
+            if w == 1:
+                nc.sync.dma_start(out=g_raw[1][:], in_=g_rows[1, :, :, 0:K_PASS])
+            for s in VECTOR_PASSES[w]:
                 for a in range(P // 32):
                     load_runs(w, s, a)
             if w in KV_VECTOR_CHUNKS:
@@ -169,7 +174,8 @@ def tile_linear_retention_pb_kernel(tc, ret_w, kv_h, Wo, bo, grad_out, out):
                         ident_f32[:],
                     )
             tokens = slice(bank * BANK_BLOCKS * P, (bank + 1) * BANK_BLOCKS * P)
-            nc.scalar.copy(out=words[:, tokens, :], in_=xt[:].rearrange("p u r -> p r u"))
+            copy = nc.scalar.copy if w == 0 else nc.vector.tensor_copy
+            copy(out=words[:, tokens, :], in_=xt[:].rearrange("p u r -> p r u"))
 
         def transpose_kv(w):
             kt = psum_t.tile([P, E_LOW, P], BF16, name="kt", tag="t")
@@ -308,7 +314,10 @@ def tile_linear_retention_pb_kernel(tc, ret_w, kv_h, Wo, bo, grad_out, out):
                 if w == 0 and s == 0:
                     widen_kv(1)
                 for half in range(2):
-                    vector_transpose(w + 1, s, half)
+                    if s in VECTOR_PASSES[w + 1]:
+                        vector_transpose(w + 1, s, half)
+                    else:
+                        transpose_g(w + 1, half, s)
                 quantise_g(w + 1, s)
             if n == WIDEN_AT_HEAD and w + 1 in KV_VECTOR_CHUNKS:
                 vector_transpose_kv(w + 1)

@@ -32,11 +32,13 @@ BANK_BLOCKS = 2
 BANKS = H_BLOCKS // BANK_BLOCKS
 
 KV_VECTOR_CHUNKS = (2, 3)
-VECTOR_PASSES = {1: (1,), 2: (0, 1), 3: (0, 1)}
+TENSOR_HALVES = {1: ((0, 0),), 2: (), 3: ()}
 VECTOR_CHUNKS = (1, 2, 3)
 RUN = 64
-STORE_GROUPS = (4, 4)
-LAST_STORE_GROUPS = (4, 2, 1)
+STORE_GROUPS = (8,)
+LAST_STORE_GROUPS = (4, 1, 1)
+END_PARTS = {1: 2, 0: 4}
+WIDE_PIECES = (2, 3)
 E_LOW = 8
 WARM_BETWEEN_LOADS = 3
 WARM_MATMULS = 5
@@ -60,7 +62,7 @@ def tile_linear_retention_pb_kernel(tc, ret_w, kv_h, Wo, bo, grad_out, out):
         keep = ctx.enter_context(tc.tile_pool(name="keep", bufs=1))
         chunk_pool = ctx.enter_context(tc.tile_pool(name="chunk", bufs=2))
         stream = ctx.enter_context(tc.tile_pool(name="stream", bufs=4))
-        out_pool = ctx.enter_context(tc.tile_pool(name="out", bufs=7))
+        out_pool = ctx.enter_context(tc.tile_pool(name="out", bufs=5))
         psum_go = ctx.enter_context(tc.psum_pool(name="psum_go", bufs=2))
         psum_t = ctx.enter_context(tc.psum_pool(name="psum_t", bufs=6))
 
@@ -72,15 +74,25 @@ def tile_linear_retention_pb_kernel(tc, ret_w, kv_h, Wo, bo, grad_out, out):
             else:
                 g_raw[w] = keep.tile([P, H_BLOCKS, K], BF16, name="g_raw%d" % w)
             if w == 1:
-                g_raw[w] = keep.tile([P, H_BLOCKS, K_PASS], BF16, name="g_raw%d" % w)
+                g_raw[w] = keep.tile([P, BANK_BLOCKS, K_PASS], BF16, name="g_raw%d" % w)
         kv_raw = [keep.tile([P, HEADS, D], BF16, name="kv_raw%d" % w, align_bytes=64) for w in range(WIDTH)]
-        wo_raw = [keep.tile([P, PACK, PASSES, PIECE_COLS], BF16, name="wo_raw%d" % i) for i in range(PIECES)]
+        wo_raw = {}
+        for piece in range(PIECES):
+            if piece not in WIDE_PIECES:
+                wo_raw[piece] = keep.tile([P, PACK, PASSES, PIECE_COLS], BF16, name="wo_raw%d" % piece)
+        wo_wide = keep.tile([P, PACK, PASSES, len(WIDE_PIECES) * PIECE_COLS], BF16, name="wo_wide")
+        for j in range(len(WIDE_PIECES)):
+            wo_raw[WIDE_PIECES[j]] = wo_wide[:, :, :, j * PIECE_COLS : (j + 1) * PIECE_COLS]
 
         def load_wo(piece, s):
             cols = slice(piece * PIECE_COLS, (piece + 1) * PIECE_COLS)
+            raw = wo_raw[piece]
+            if piece in WIDE_PIECES:
+                cols = slice(WIDE_PIECES[0] * PIECE_COLS, (WIDE_PIECES[-1] + 1) * PIECE_COLS)
+                raw = wo_wide
             for u in range(HALVES):
                 nc.sync.dma_start(
-                    out=wo_raw[piece][:, PAIR * u : PAIR * (u + 1), s, :],
+                    out=raw[:, PAIR * u : PAIR * (u + 1), s, :],
                     in_=wo_rows[s, u, :, :, cols],
                 )
 
@@ -88,12 +100,12 @@ def tile_linear_retention_pb_kernel(tc, ret_w, kv_h, Wo, bo, grad_out, out):
             blocks = slice(bank * BANK_BLOCKS, (bank + 1) * BANK_BLOCKS)
             nc.sync.dma_start(out=g_raw[w][:, blocks, :], in_=g_rows[w, :, blocks, :])
 
-        def load_runs(w, s, a):
+        def load_runs(w, s, a, half):
             for u in range(HALVES):
                 first = s * K_PASS + u * PAIR * P + a * RUN
                 nc.sync.dma_start(
-                    out=x_t[w][32 * a + u : 32 * (a + 1) : HALVES, s, :].rearrange("p (b k) -> p b k", k=RUN),
-                    in_=g_runs[w, :, :, first : first + RUN],
+                    out=x_t[w][32 * a + u : 32 * (a + 1) : HALVES, s, half * HEIGHT * PACK // 2 :].rearrange("p (b k) -> p b k", k=RUN),
+                    in_=g_runs[w, :, half * HEIGHT // 32 :, first : first + RUN],
                 )
 
         def load_kv(w):
@@ -113,15 +125,15 @@ def tile_linear_retention_pb_kernel(tc, ret_w, kv_h, Wo, bo, grad_out, out):
         for w in range(WIDTH):
             if w not in KV_VECTOR_CHUNKS:
                 load_kv(w)
-        for piece in range(1, PIECES):
+        for piece in range(1, PIECES - 1):
             for s in range(PASSES):
                 load_wo(piece, s)
         for w in VECTOR_CHUNKS:
             if w == 1:
-                nc.sync.dma_start(out=g_raw[1][:], in_=g_rows[1, :, :, 0:K_PASS])
-            for s in VECTOR_PASSES[w]:
+                nc.sync.dma_start(out=g_raw[1][:], in_=g_rows[1, :, 0:BANK_BLOCKS, 0:K_PASS])
+            for s in range(PASSES):
                 for a in range(P // 32):
-                    load_runs(w, s, a)
+                    load_runs(w, s, a, int((0, s) in TENSOR_HALVES[w]))
             if w in KV_VECTOR_CHUNKS:
                 load_kv_runs(w)
 
@@ -146,8 +158,8 @@ def tile_linear_retention_pb_kernel(tc, ret_w, kv_h, Wo, bo, grad_out, out):
         def prepare_wo(piece):
             grouped = chunk_pool.tile([P, PASSES * PIECE_COLS, PACK], BF16, name="wo_grouped", align_bytes=64)
             nc.vector.tensor_copy(
-                out=grouped[:].rearrange("p (c i) t -> p c t i", i=4),
-                in_=wo_raw[piece][:].rearrange("p t s (c i) -> p (s c) t i", i=4),
+                out=grouped[:].rearrange("p (s c i) t -> p s c t i", s=PASSES, i=4),
+                in_=wo_raw[piece][:].rearrange("p t s (c i) -> p s c t i", i=4),
             )
             nc.vector.quantize_mx(
                 out=wo_codes[piece][:].rearrange("p s c -> p (s c)").bitcast(E4M3_X4),
@@ -266,20 +278,24 @@ def tile_linear_retention_pb_kernel(tc, ret_w, kv_h, Wo, bo, grad_out, out):
                         nc.sync.dma_start(out=out_rows[w, :, :, first : first + size, :], in_=store_tiles[w][:])
                 first += size
 
-        def read_out_last(w, n, go_sb):
+        def read_out_last(w, n, go_sb, parts):
             kv_t = kv_wide[w]
-            for hb in range(H_BLOCKS):
-                out_ps = psum_t.tile([P, D], F32, name="out_ps_block", tag="t")
-                nc.tensor.matmul(
-                    out=out_ps[:], lhsT=go_sb[:, hb * P : (hb + 1) * P], rhs=kv_t[:, n, :], start=True, stop=True
-                )
-                out_sb = out_pool.tile([P, D], F32, name="out_sb_block")
-                if hb % 2 == 0:
+            blocks = H_BLOCKS // parts
+            for part in range(parts):
+                out_ps = psum_t.tile([P, blocks, D], F32, name="out_ps_part", tag="t")
+                for b in range(blocks):
+                    hb = part * blocks + b
+                    nc.tensor.matmul(
+                        out=out_ps[:, b, :], lhsT=go_sb[:, hb * P : (hb + 1) * P], rhs=kv_t[:, n, :], start=True, stop=True
+                    )
+                out_sb = out_pool.tile([P, blocks, D], F32, name="out_sb_part%d" % parts)
+                rows = out_rows[w, :, part * blocks : (part + 1) * blocks, n, :]
+                if part % 2 == 0:
                     nc.scalar.copy(out=out_sb[:], in_=out_ps[:])
-                    nc.scalar.dma_start(out=out_rows[w, :, hb, n, :], in_=out_sb[:])
+                    nc.scalar.dma_start(out=rows, in_=out_sb[:])
                 else:
                     nc.vector.tensor_copy(out=out_sb[:], in_=out_ps[:])
-                    nc.sync.dma_start(out=out_rows[w, :, hb, n, :], in_=out_sb[:])
+                    nc.sync.dma_start(out=rows, in_=out_sb[:])
 
         steps = [(w, n) for w in range(WIDTH) for n in range(HEADS)]
         prepare_wo(0)
@@ -303,10 +319,11 @@ def tile_linear_retention_pb_kernel(tc, ret_w, kv_h, Wo, bo, grad_out, out):
             if i + 1 < len(steps) and i + 1 not in go:
                 go[i + 1] = project(steps[i + 1][0], steps[i + 1][1])
             go_now = go[i]
-            if i + 1 < len(steps):
-                read_out(w, n, go_now)
+            from_end = len(steps) - 1 - i
+            if from_end in END_PARTS:
+                read_out_last(w, n, go_now, END_PARTS[from_end])
             else:
-                read_out_last(w, n, go_now)
+                read_out(w, n, go_now)
             if w == 0 and n % PIECE_HEADS == 0 and n // PIECE_HEADS + PIECES_AHEAD < PIECES:
                 prepare_wo(n // PIECE_HEADS + PIECES_AHEAD)
             if w + 1 < WIDTH and n in PREPARE_AT_HEADS:
@@ -314,7 +331,7 @@ def tile_linear_retention_pb_kernel(tc, ret_w, kv_h, Wo, bo, grad_out, out):
                 if w == 0 and s == 0:
                     widen_kv(1)
                 for half in range(2):
-                    if s in VECTOR_PASSES[w + 1]:
+                    if (half, s) not in TENSOR_HALVES[w + 1]:
                         vector_transpose(w + 1, s, half)
                     else:
                         transpose_g(w + 1, half, s)

from contextlib import ExitStack

import concourse.mybir as mybir
from concourse.masks import make_identity

F32 = mybir.dt.float32
BF16 = mybir.dt.bfloat16
U32 = mybir.dt.uint32
U8 = mybir.dt.uint8
E4M3_X4 = mybir.dt.float8_e4m3fn_x4
E5M2_X4 = mybir.dt.float8_e5m2_x4

P = 128
PACK = 4
PAIR = 2
HALVES = PACK // PAIR
K_PASS = P * PACK

HEIGHT, WIDTH, HEADS, D = 512, 4, 8, 128
K = 1024
PASSES = K // K_PASS
H_BLOCKS = HEIGHT // P

PIECE_HEADS = 2
PIECE_COLS = PIECE_HEADS * D
PIECES = HEADS // PIECE_HEADS
PIECES_AHEAD = 2
PREPARE_AT_HEADS = (3, 5)
WIDEN_AT_HEAD = 6
GO_PARTS = 2
BANK_BLOCKS = 2
BANKS = H_BLOCKS // BANK_BLOCKS

KV_VECTOR_CHUNKS = (2, 3)
TENSOR_HALVES = {1: ((0, 0),), 2: (), 3: ()}
VECTOR_CHUNKS = (1, 2, 3)
RUN = 64
STORE_GROUPS = (8,)
LAST_STORE_GROUPS = (4, 1, 1)
END_PARTS = {1: 2, 0: 4}
WIDE_PIECES = (2, 3)
E_LOW = 8
WARM_BETWEEN_LOADS = 3
WARM_MATMULS = 5

FLOPS = 2 * HEIGHT * WIDTH * K * HEADS * D + 2 * HEIGHT * WIDTH * HEADS * D * D
BYTES = 2 * (WIDTH * HEADS * D * D + K * HEADS * D + HEIGHT * WIDTH * K) + 4 * HEIGHT * WIDTH * HEADS * D


def tile_linear_retention_pb_kernel(tc, ret_w, kv_h, Wo, bo, grad_out, out):
    nc = tc.nc

    g_rows = grad_out[0].rearrange("(hb p w) k -> w p hb k", hb=H_BLOCKS, p=P, w=WIDTH)
    g_runs = grad_out[0].rearrange("(b r w) k -> w r b k", b=HEIGHT // 16, r=16, w=WIDTH)
    kv_runs = kv_h[0].rearrange("w n (eh j) (a i) -> w a j (n eh) i", eh=D // 32, j=32, a=D // 32, i=32)
    kv_rows = kv_h[0].rearrange("w n (eh el) f -> w (n eh) (el f)", el=E_LOW)
    wo_rows = Wo.rearrange("(s u p e) c -> s u p e c", s=PASSES, u=HALVES, p=P, e=PAIR)
    out_rows = out[0].rearrange("(hb p) w n e -> w p hb n e", hb=H_BLOCKS, p=P)

    with ExitStack() as ctx:
        ctx.enter_context(tc.manual_schedule())
        keep = ctx.enter_context(tc.tile_pool(name="keep", bufs=1))
        chunk_pool = ctx.enter_context(tc.tile_pool(name="chunk", bufs=2))
        stream = ctx.enter_context(tc.tile_pool(name="stream", bufs=4))
        out_pool = ctx.enter_context(tc.tile_pool(name="out", bufs=5))
        psum_go = ctx.enter_context(tc.psum_pool(name="psum_go", bufs=2))
        psum_t = ctx.enter_context(tc.psum_pool(name="psum_t", bufs=6))

        g_raw = {}
        x_t = {}
        for w in range(WIDTH):
            if w in VECTOR_CHUNKS:
                x_t[w] = keep.tile([P, PASSES, HEIGHT * PACK], BF16, name="x_t%d" % w, align_bytes=64)
            else:
                g_raw[w] = keep.tile([P, H_BLOCKS, K], BF16, name="g_raw%d" % w)
            if w == 1:
                g_raw[w] = keep.tile([P, BANK_BLOCKS, K_PASS], BF16, name="g_raw%d" % w)
        kv_raw = [keep.tile([P, HEADS, D], BF16, name="kv_raw%d" % w, align_bytes=64) for w in range(WIDTH)]
        wo_raw = {}
        for piece in range(PIECES):
            if piece not in WIDE_PIECES:
                wo_raw[piece] = keep.tile([P, PACK, PASSES, PIECE_COLS], BF16, name="wo_raw%d" % piece)
        wo_wide = keep.tile([P, PACK, PASSES, len(WIDE_PIECES) * PIECE_COLS], BF16, name="wo_wide")
        for j in range(len(WIDE_PIECES)):
            wo_raw[WIDE_PIECES[j]] = wo_wide[:, :, :, j * PIECE_COLS : (j + 1) * PIECE_COLS]

        def load_wo(piece, s):
            cols = slice(piece * PIECE_COLS, (piece + 1) * PIECE_COLS)
            raw = wo_raw[piece]
            if piece in WIDE_PIECES:
                cols = slice(WIDE_PIECES[0] * PIECE_COLS, (WIDE_PIECES[-1] + 1) * PIECE_COLS)
                raw = wo_wide
            for u in range(HALVES):
                nc.sync.dma_start(
                    out=raw[:, PAIR * u : PAIR * (u + 1), s, :],
                    in_=wo_rows[s, u, :, :, cols],
                )

        def load_g_bank(w, bank):
            blocks = slice(bank * BANK_BLOCKS, (bank + 1) * BANK_BLOCKS)
            nc.sync.dma_start(out=g_raw[w][:, blocks, :], in_=g_rows[w, :, blocks, :])

        def load_runs(w, s, a, half):
            for u in range(HALVES):
                first = s * K_PASS + u * PAIR * P + a * RUN
                nc.sync.dma_start(
                    out=x_t[w][32 * a + u : 32 * (a + 1) : HALVES, s, half * HEIGHT * PACK // 2 :].rearrange("p (b k) -> p b k", k=RUN),
                    in_=g_runs[w, :, half * HEIGHT // 32 :, first : first + RUN],
                )

        def load_kv(w):
            nc.sync.dma_start(out=kv_raw[w][:].rearrange("p el f -> p (el f)"), in_=kv_rows[w])

        def load_kv_runs(w):
            for a in range(P // 32):
                nc.sync.dma_start(
                    out=kv_raw[w][32 * a : 32 * (a + 1), :, :].rearrange("p n (eh i) -> p (n eh) i", i=32),
                    in_=kv_runs[w, a],
                )

        load_g_bank(0, 0)
        for s in range(PASSES):
            load_wo(0, s)
        load_g_bank(0, 1)
        for w in range(WIDTH):
            if w not in KV_VECTOR_CHUNKS:
                load_kv(w)
        for piece in range(1, PIECES - 1):
            for s in range(PASSES):
                load_wo(piece, s)
        for w in VECTOR_CHUNKS:
            if w == 1:
                nc.sync.dma_start(out=g_raw[1][:], in_=g_rows[1, :, 0:BANK_BLOCKS, 0:K_PASS])
            for s in range(PASSES):
                for a in range(P // 32):
                    load_runs(w, s, a, int((0, s) in TENSOR_HALVES[w]))
            if w in KV_VECTOR_CHUNKS:
                load_kv_runs(w)

        warm_sb = keep.tile([P, HEIGHT], BF16, name="warm_sb")
        nc.vector.memset(warm_sb[:], 0.0)
        warm_ps = psum_t.tile([P, HEIGHT], F32, name="warm_ps", tag="t")

        def warm(count):
            for i in range(count):
                nc.tensor.matmul(out=warm_ps[:], lhsT=warm_sb[:, :P], rhs=warm_sb[:], start=True, stop=True)

        warm(WARM_MATMULS)

        ident_f32 = keep.tile([P, P], F32, name="ident_f32")
        make_identity(nc, ident_f32[:])
        ident_bf16 = keep.tile([P, P], BF16, name="ident_bf16")
        make_identity(nc, ident_bf16[:])

        wo_codes = [keep.tile([P, PASSES, PIECE_COLS], U32, name="wo_codes%d" % i, align_bytes=64) for i in range(PIECES)]
        wo_scales = [keep.tile([P, PASSES, PIECE_COLS], U8, name="wo_scales%d" % i, align_bytes=64) for i in range(PIECES)]

        def prepare_wo(piece):
            grouped = chunk_pool.tile([P, PASSES * PIECE_COLS, PACK], BF16, name="wo_grouped", align_bytes=64)
            nc.vector.tensor_copy(
                out=grouped[:].rearrange("p (s c i) t -> p s c t i", s=PASSES, i=4),
                in_=wo_raw[piece][:].rearrange("p t s (c i) -> p s c t i", i=4),
            )
            nc.vector.quantize_mx(
                out=wo_codes[piece][:].rearrange("p s c -> p (s c)").bitcast(E4M3_X4),
                scales=wo_scales[piece][:].rearrange("p s c -> p (s c)"),
                in_=grouped[:].rearrange("p c t -> p (c t)"),
            )

        g_grouped = {}
        kv_wide = {}
        kv_turned = {}
        chunk = {}

        def transpose_g(w, bank, s):
            if w not in g_grouped:
                g_grouped[w] = chunk_pool.tile([P, PASSES, HEIGHT * PACK], BF16, name="g_grouped", align_bytes=64)
            words = g_grouped[w][:, s, :].bitcast(F32).rearrange("p (r u) -> p r u", u=HALVES)
            xt = psum_t.tile([P, HALVES, BANK_BLOCKS * P], F32, name="xt", tag="t")
            for u in range(HALVES):
                first = (s * HALVES + u) * P
                for b in range(BANK_BLOCKS):
                    nc.tensor.transpose(
                        xt[:, u, b * P : (b + 1) * P],
                        g_raw[w][:, bank * BANK_BLOCKS + b, :].bitcast(F32)[:, first : first + P],
                        ident_f32[:],
                    )
            tokens = slice(bank * BANK_BLOCKS * P, (bank + 1) * BANK_BLOCKS * P)
            copy = nc.scalar.copy if w == 0 else nc.vector.tensor_copy
            copy(out=words[:, tokens, :], in_=xt[:].rearrange("p u r -> p r u"))

        def transpose_kv(w):
            kt = psum_t.tile([P, E_LOW, P], BF16, name="kt", tag="t")
            for el in range(E_LOW):
                nc.tensor.transpose(kt[:, el, :], kv_raw[w][:, el, :], ident_bf16[:])
            kv_turned[w] = kt

        def vector_transpose(w, s, half):
            if w not in g_grouped:
                g_grouped[w] = chunk_pool.tile([P, PASSES, HEIGHT * PACK], BF16, name="g_grouped", align_bytes=64)
            cols = slice(half * HEIGHT * PACK // 2, (half + 1) * HEIGHT * PACK // 2)
            nc.vector.transpose(out=g_grouped[w][:, s, cols].bitcast(F32), in_=x_t[w][:, s, cols].bitcast(F32))

        def vector_transpose_kv(w):
            kt = chunk_pool.tile([P, HEADS, D], BF16, name="kt_sb", align_bytes=64)
            nc.vector.transpose(
                out=kt[:].rearrange("p n e -> p (n e)"), in_=kv_raw[w][:].rearrange("p n e -> p (n e)")
            )
            kv_turned[w] = kt

        def quantise_g(w, s):
            if w not in chunk:
                codes = chunk_pool.tile([P, PASSES, HEIGHT], U32, name="g_codes", align_bytes=64)
                scales = chunk_pool.tile([P, PASSES, HEIGHT], U8, name="g_scales", align_bytes=64)
                chunk[w] = [codes, scales, None]
            nc.vector.quantize_mx(
                out=chunk[w][0][:, s, :].bitcast(E5M2_X4), scales=chunk[w][1][:, s, :], in_=g_grouped[w][:, s, :]
            )

        def widen_kv(w):
            kv_t = chunk_pool.tile([P, HEADS, D], F32, name="kv_t")
            copy = nc.scalar.copy if w == 0 else nc.vector.tensor_copy
            if w in KV_VECTOR_CHUNKS:
                copy(out=kv_t[:], in_=kv_turned[w][:])
            else:
                copy(
                    out=kv_t[:].rearrange("p n (eh el) -> p (n eh) el", el=E_LOW),
                    in_=kv_turned[w][:].rearrange("p el q -> p q el"),
                )
            kv_wide[w] = kv_t

        def mx_pass(w, n, s, go_ps):
            piece = n // PIECE_HEADS
            cols = slice((n % PIECE_HEADS) * D, (n % PIECE_HEADS + 1) * D)
            nc.tensor.matmul_mx(
                out=go_ps[:],
                lhsT=wo_codes[piece][:, s, cols].bitcast(E4M3_X4),
                lhsT_scale=wo_scales[piece][:, s, cols],
                rhs=chunk[w][0][:, s, :].bitcast(E5M2_X4),
                rhs_scale=chunk[w][1][:, s, :],
                start=(s == 0),
                stop=(s == PASSES - 1),
            )

        def copy_go(go_ps):
            go_sb = stream.tile([P, HEIGHT], F32, name="go_sb")
            for part in range(GO_PARTS):
                tokens = slice(part * HEIGHT // GO_PARTS, (part + 1) * HEIGHT // GO_PARTS)
                nc.scalar.copy(out=go_sb[:, tokens], in_=go_ps[:, tokens])
            return go_sb

        def project(w, n):
            go_ps = psum_go.tile([P, HEIGHT], F32, name="go_ps")
            for s in range(PASSES):
                mx_pass(w, n, s, go_ps)
            return copy_go(go_ps)

        store_tiles = {}

        def read_out(w, n, go_sb):
            kv_t = kv_wide[w]
            out_ps = psum_t.tile([P, H_BLOCKS, D], F32, name="out_ps", tag="t")
            for hb in range(H_BLOCKS):
                nc.tensor.matmul(
                    out=out_ps[:, hb, :],
                    lhsT=go_sb[:, hb * P : (hb + 1) * P],
                    rhs=kv_t[:, n, :],
                    start=True,
                    stop=True,
                )
            first = 0
            for size in (LAST_STORE_GROUPS if w == WIDTH - 1 else STORE_GROUPS):
                if first <= n < first + size:
                    if n == first:
                        store_tiles[w] = out_pool.tile([P, H_BLOCKS, size, D], F32, name="out_sb")
                    nc.scalar.copy(out=store_tiles[w][:, :, n - first, :], in_=out_ps[:])
                    if n == first + size - 1:
                        nc.sync.dma_start(out=out_rows[w, :, :, first : first + size, :], in_=store_tiles[w][:])
                first += size

        def read_out_last(w, n, go_sb, parts):
            kv_t = kv_wide[w]
            blocks = H_BLOCKS // parts
            for part in range(parts):
                out_ps = psum_t.tile([P, blocks, D], F32, name="out_ps_part", tag="t")
                for b in range(blocks):
                    hb = part * blocks + b
                    nc.tensor.matmul(
                        out=out_ps[:, b, :], lhsT=go_sb[:, hb * P : (hb + 1) * P], rhs=kv_t[:, n, :], start=True, stop=True
                    )
                out_sb = out_pool.tile([P, blocks, D], F32, name="out_sb_part%d" % parts)
                rows = out_rows[w, :, part * blocks : (part + 1) * blocks, n, :]
                if part % 2 == 0:
                    nc.scalar.copy(out=out_sb[:], in_=out_ps[:])
                    nc.scalar.dma_start(out=rows, in_=out_sb[:])
                else:
                    nc.vector.tensor_copy(out=out_sb[:], in_=out_ps[:])
                    nc.sync.dma_start(out=rows, in_=out_sb[:])

        steps = [(w, n) for w in range(WIDTH) for n in range(HEADS)]
        prepare_wo(0)
        for bank in range(BANKS):
            for s in range(PASSES):
                transpose_g(0, bank, s)
            if bank == 0:
                warm(WARM_BETWEEN_LOADS)
        for w in range(WIDTH):
            if w not in KV_VECTOR_CHUNKS:
                transpose_kv(w)
                warm(1)
        widen_kv(0)
        for s in range(PASSES):
            quantise_g(0, s)
        go = {0: project(0, 0)}
        for piece in range(1, PIECES_AHEAD):
            prepare_wo(piece)
        for i in range(len(steps)):
            w, n = steps[i]
            if i + 1 < len(steps) and i + 1 not in go:
                go[i + 1] = project(steps[i + 1][0], steps[i + 1][1])
            go_now = go[i]
            from_end = len(steps) - 1 - i
            if from_end in END_PARTS:
                read_out_last(w, n, go_now, END_PARTS[from_end])
            else:
                read_out(w, n, go_now)
            if w == 0 and n % PIECE_HEADS == 0 and n // PIECE_HEADS + PIECES_AHEAD < PIECES:
                prepare_wo(n // PIECE_HEADS + PIECES_AHEAD)
            if w + 1 < WIDTH and n in PREPARE_AT_HEADS:
                s = PREPARE_AT_HEADS.index(n)
                if w == 0 and s == 0:
                    widen_kv(1)
                for half in range(2):
                    if (half, s) not in TENSOR_HALVES[w + 1]:
                        vector_transpose(w + 1, s, half)
                    else:
                        transpose_g(w + 1, half, s)
                quantise_g(w + 1, s)
            if n == WIDEN_AT_HEAD and w + 1 in KV_VECTOR_CHUNKS:
                vector_transpose_kv(w + 1)
                widen_kv(w + 1)
